import numpy as np
import ml_dtypes


def mxq(x, axis, fmt="e4m3"):
    dtype, down = {"e4m3": (ml_dtypes.float8_e4m3fn, 7), "e5m2": (ml_dtypes.float8_e5m2, 14)}[fmt]
    v = np.moveaxis(np.asarray(x, np.float32).astype(ml_dtypes.bfloat16).astype(np.float64), axis, -1)
    blocks = v.reshape(v.shape[:-1] + (-1, 32))
    amax = np.abs(blocks).max(-1, keepdims=True)
    byte = np.maximum(np.where(amax > 0, np.frexp(amax)[1] - 1 + 127, 0) - down, 1)
    scale = np.exp2(byte - 127.0)
    codes = (blocks / scale).astype(np.float32).astype(dtype).astype(np.float64)
    return np.moveaxis((codes * scale).reshape(v.shape), -1, axis)


WIDE = False


def mx_kscale(k):
    if not WIDE:
        return np.ones(k)
    levels = np.array([10, -10, 5, -5, 0])
    if k % 512:
        return np.exp2(np.random.permutation(np.resize(levels, k // 32))).repeat(32)
    a = np.empty((k // 512, 16))
    for p in range(k // 512):
        a[p, :8] = np.random.permutation(np.resize(levels, 8))
        for g in range(8):
            far = levels[np.abs(levels - a[p, g]) >= 10]
            a[p, g + 8] = far[np.random.randint(len(far))]
    return np.exp2(a.ravel()).repeat(32)


BF16 = ml_dtypes.bfloat16


def bf(x):
    return np.asarray(x, np.float32).astype(BF16)


def f64(x):
    return np.asarray(x).astype(np.float64)


N, D = 512, 512
C_IN = 1.0
C_OUT = 1.0
EPS = 1e-15
BOUND = 1.0 - 168.0 * 2.0 ** -24
LN_EPS = 1e-5


def atanh(z):
    return 0.5 * np.log((1.0 + z) / (1.0 - z))


def _norm(x):
    return np.clip(np.linalg.norm(x, axis=-1, keepdims=True), EPS, None)


def logmap0(x, c):
    sc = c ** 0.5
    n = _norm(x)
    return atanh(np.clip(sc * n, None, BOUND)) * x / (sc * n)


def expmap0(u, c):
    sc = c ** 0.5
    n = _norm(u)
    return np.tanh(sc * n) * u / (sc * n)


def mobius_add(x, y, c):
    x2 = np.sum(x * x, -1, keepdims=True)
    y2 = np.sum(y * y, -1, keepdims=True)
    xy = np.sum(x * y, -1, keepdims=True)
    num = (1.0 + 2.0 * c * xy + c * y2) * x + (1.0 - c * x2) * y
    den = 1.0 + 2.0 * c * xy + (c * c) * x2 * y2
    return num / np.clip(den, EPS, None)


def expmap(x, u, c):
    sc = c ** 0.5
    n = _norm(u)
    lam = 2.0 / np.clip(1.0 - c * np.sum(x * x, -1, keepdims=True), EPS, None)
    second = np.tanh(sc * lam * n / 2.0) * u / (sc * n)
    return mobius_add(x, second, c)


def transp0(y, v, c):
    return v * (1.0 - c * np.sum(y * y, -1, keepdims=True))


def setup_inputs():
    s = mx_kscale(D)
    s = s / np.sqrt(np.mean(s * s))
    c = np.random.uniform(0.5, 0.8, (N, 1))
    far = np.random.uniform(0.0, 1.0, (N, 1)) < 0.5
    tau = np.where(far, np.random.uniform(1.5, 2.0, (N, 1)), np.exp(np.random.uniform(np.log(0.04), np.log(0.1), (N, 1))))
    h = c / np.sqrt(D) + tau * np.sqrt(LN_EPS) * np.random.standard_normal((N, D))
    gamma = 12.0 / np.sqrt(D) * (1.0 + 0.1 * np.random.standard_normal(D)) * s
    beta = 0.8 / np.sqrt(D) * np.random.standard_normal(D) * s
    weight = 0.25 / np.sqrt(D) * np.random.standard_normal((D, D)) / s[None, :]
    bias = 0.4 / np.sqrt(D) * np.random.standard_normal((1, D))
    return {'h': bf(h), 'weight': bf(weight), 'bias': bf(bias), 'gamma': bf(gamma), 'beta': bf(beta)}


def reference(h, weight, bias, gamma, beta):
    x = logmap0(f64(h), C_IN)
    mu = np.mean(x, -1, keepdims=True)
    var = np.mean((x - mu) ** 2, -1, keepdims=True)
    x = (x - mu) * (1.0 / np.sqrt(var + LN_EPS)) * f64(gamma) + f64(beta)
    hn = expmap0(x, C_IN)
    u = logmap0(hn, C_IN)
    xt = mxq(u, 1, 'e4m3') @ mxq(f64(weight), 1, 'e4m3').T
    res = expmap0(xt, C_IN)
    b = transp0(res, f64(bias), C_IN)
    res = expmap(res, b, C_IN)
    return expmap0(np.maximum(logmap0(res, C_IN), 0.0), C_OUT)

@@ -1,0 +1,524 @@
+import math
+from contextlib import ExitStack
+
+import concourse.mybir as mybir
+from concourse.masks import make_identity
+
+F32 = mybir.dt.float32
+BF16 = mybir.dt.bfloat16
+U32 = mybir.dt.uint32
+U8 = mybir.dt.uint8
+FP8X4 = mybir.dt.float8_e4m3fn_x4
+ALU = mybir.AluOpType
+ACT = mybir.ActivationFunctionType
+
+P = 128
+PACK = 4
+N_ROWS = 512
+D = 512
+TILES = N_ROWS // P
+
+BOUND = 1.0 - 168.0 * 2.0 ** -24
+ARTANH_BOUND = 0.5 * math.log((1.0 + BOUND) / (1.0 - BOUND))
+LN_EPS = 1e-5
+NORM_MIN = 1e-15
+NORM_MIN_SQ = 1e-30
+SUM_SQ_MIN = 1e-20
+
+FLOPS = 2 * N_ROWS * D * D
+
+
+def tile_hnnlayer_s_kernel(tc, h, weight, bias, gamma, beta, out):
+    nc = tc.nc
+    with ExitStack() as ctx:
+        keep = ctx.enter_context(tc.tile_pool(name="keep", bufs=1))
+        scrap = ctx.enter_context(tc.tile_pool(name="scrap", bufs=4))
+        psum_tr = ctx.enter_context(tc.psum_pool(name="psum_tr", bufs=4))
+        psum_xt = ctx.enter_context(tc.psum_pool(name="psum_xt", bufs=1))
+        ctx.enter_context(tc.manual_schedule())
+
+        def per_tile(shape, dtype, name):
+            return [
+                keep.tile(shape, dtype, name="%s%d" % (name, i), align_bytes=64)
+                for i in range(TILES)
+            ]
+
+        def row_numbers(name):
+            return keep.tile([P, TILES], F32, name=name)
+
+        def one_number(name):
+            return keep.tile([P, 1], F32, name=name)
+
+        def cols(rows):
+            return slice(rows[0], rows[-1] + 1)
+
+        def power(dst, src, exponent, rows):
+            c = cols(rows)
+            nc.gpsimd.tensor_tensor(out=dst[:, c], in0=src[:, c], in1=exponent[:, c], op=ALU.pow)
+
+        def load_table(func, name):
+            unused = one_number(name)
+            nc.scalar.activation(out=unused[:], in_=ones[:], func=func)
+
+        def square_sum(src, total):
+            squares = scrap.tile([P, D], BF16, name="squares")
+            nc.scalar.activation(out=squares[:], in_=src, func=ACT.Square, accum_out=total)
+
+        h_sb = keep.tile([P, TILES, D], BF16, name="h_sb")
+        for i in range(TILES):
+            nc.sync.dma_start(out=h_sb[:, i, :], in_=h[i * P : (i + 1) * P, :])
+        w_sb = keep.tile([P, TILES, D], BF16, name="w_sb")
+        nc.sync.dma_start(out=w_sb[:], in_=weight.rearrange("(o p) k -> p o k", p=P))
+        gamma_bc = keep.tile([P, D], BF16, name="gamma_bc")
+        nc.sync.dma_start(out=gamma_bc[:], in_=gamma.partition_broadcast(P))
+        bias_bc = keep.tile([P, D], BF16, name="bias_bc")
+        nc.sync.dma_start(
+            out=bias_bc[:], in_=bias.rearrange("o d -> (o d)").partition_broadcast(P)
+        )
+        beta_bc = keep.tile([P, D], BF16, name="beta_bc")
+        nc.sync.dma_start(out=beta_bc[:], in_=beta.partition_broadcast(P))
+
+        half = row_numbers("half")
+        nc.vector.memset(half[:], 0.5)
+        neg_half = row_numbers("neg_half")
+        nc.vector.memset(neg_half[:], -0.5)
+        ones = one_number("ones")
+        nc.vector.memset(ones[:], 1.0)
+        ident = keep.tile([P, P], BF16, name="ident")
+        make_identity(nc, ident[:])
+        load_table(ACT.Ln, "warm_ln_a")
+
+        first = h_sb[:, :, 0]
+        d = per_tile([P, D], F32, "d")
+        d_sum = row_numbers("d_sum")
+        d_sq = row_numbers("d_sq")
+
+        def shifted_sums(rows):
+            for i in rows:
+                squares = scrap.tile([P, D], BF16, name="squares")
+                nc.scalar.activation(
+                    out=squares[:], in_=h_sb[:, i, :], func=ACT.Square, scale=-1.0,
+                    bias=h_sb[:, i, 0:1], accum_out=d_sq[:, i : i + 1],
+                )
+                nc.vector.tensor_scalar(
+                    out=d[i][:], in0=h_sb[:, i, :], scalar1=h_sb[:, i, 0:1], scalar2=None,
+                    op0=ALU.subtract, op1=ALU.add, accum_out=d_sum[:, i : i + 1],
+                )
+
+        first_x2 = row_numbers("first_x2")
+        first_sq = row_numbers("first_sq")
+        h_sq_a = row_numbers("h_sq_a")
+        h_sq_b = row_numbers("h_sq_b")
+        h_sq = row_numbers("h_sq")
+        h_norm = row_numbers("h_norm")
+        h_clip = row_numbers("h_clip")
+        d_mean = row_numbers("d_mean")
+
+        def first_terms(rows):
+            c = cols(rows)
+            nc.vector.tensor_scalar_mul(out=first_x2[:, c], in0=first[:, c], scalar1=2.0)
+            nc.vector.scalar_tensor_tensor(
+                out=first_sq[:, c], in0=first[:, c], scalar=1.0 * D, in1=first[:, c],
+                op0=ALU.mult, op1=ALU.mult,
+            )
+
+        def norm_of_h(rows):
+            c = cols(rows)
+            nc.vector.tensor_add(out=h_sq_a[:, c], in0=d_sq[:, c], in1=first_sq[:, c])
+            nc.vector.tensor_mul(out=h_sq_b[:, c], in0=d_sum[:, c], in1=first_x2[:, c])
+            nc.vector.tensor_add(out=h_sq[:, c], in0=h_sq_a[:, c], in1=h_sq_b[:, c])
+            power(h_norm, h_sq, half, rows)
+            nc.gpsimd.tensor_scalar_min(out=h_clip[:, c], in0=h_norm[:, c], scalar1=BOUND)
+            nc.vector.tensor_scalar_mul(out=d_mean[:, c], in0=d_sum[:, c], scalar1=1.0 / D)
+
+        centred = per_tile([P, D], F32, "centred")
+
+        def centre(rows):
+            for i in rows:
+                nc.vector.scalar_tensor_tensor(
+                    out=centred[i][:], in0=d[i][:], scalar=d_mean[:, i : i + 1],
+                    in1=gamma_bc[:], op0=ALU.subtract, op1=ALU.mult,
+                )
+
+        d_sum_mean = row_numbers("d_sum_mean")
+        dev_sq = row_numbers("dev_sq")
+        eps_h_sq = row_numbers("eps_h_sq")
+        quarter_var = row_numbers("quarter_var")
+
+        def variance(rows):
+            c = cols(rows)
+            nc.vector.tensor_mul(out=d_sum_mean[:, c], in0=d_sum[:, c], in1=d_mean[:, c])
+            nc.vector.tensor_sub(out=dev_sq[:, c], in0=d_sq[:, c], in1=d_sum_mean[:, c])
+            nc.vector.tensor_scalar(
+                out=eps_h_sq[:, c], in0=h_sq[:, c], scalar1=NORM_MIN_SQ, scalar2=LN_EPS,
+                op0=ALU.max, op1=ALU.mult,
+            )
+            nc.vector.tensor_scalar_mul(out=quarter_var[:, c], in0=dev_sq[:, c], scalar1=0.25 / D)
+
+        ln_up = row_numbers("ln_up")
+        ln_dn = row_numbers("ln_dn")
+
+        def log_of_h(rows):
+            c = cols(rows)
+            nc.scalar.activation(out=ln_up[:, c], in_=h_clip[:, c], func=ACT.Ln, bias=1.0, scale=1.0)
+            nc.scalar.activation(out=ln_dn[:, c], in_=h_clip[:, c], func=ACT.Ln, bias=1.0, scale=-1.0)
+
+        theta2 = row_numbers("theta2")
+        theta_sq = row_numbers("theta_sq")
+        k_arg = row_numbers("k_arg")
+        k_rsqrt = row_numbers("k_rsqrt")
+        k = row_numbers("k")
+
+        def layer_norm_scale(rows):
+            c = cols(rows)
+            for i in rows:
+                nc.scalar.activation(
+                    out=theta_sq[:, i : i + 1], in_=ln_dn[:, i : i + 1], func=ACT.Square,
+                    scale=-1.0, bias=ln_up[:, i : i + 1],
+                )
+            for i in rows:
+                nc.scalar.activation(
+                    out=k_arg[:, i : i + 1], in_=theta_sq[:, i : i + 1], func=ACT.Identity,
+                    scale=quarter_var[:, i : i + 1], bias=eps_h_sq[:, i : i + 1],
+                )
+            power(k_rsqrt, k_arg, neg_half, rows)
+            nc.vector.tensor_sub(out=theta2[:, c], in0=ln_up[:, c], in1=ln_dn[:, c])
+
+        x = per_tile([P, D], F32, "x")
+        x_sq = row_numbers("x_sq")
+        x_rnorm = row_numbers("x_rnorm")
+
+        def layer_norm_factor(rows):
+            c = cols(rows)
+            nc.vector.scalar_tensor_tensor(
+                out=k[:, c], in0=theta2[:, c], scalar=0.5, in1=k_rsqrt[:, c],
+                op0=ALU.mult, op1=ALU.mult,
+            )
+
+        def layer_norm(rows):
+            for i in rows:
+                nc.vector.scalar_tensor_tensor(
+                    out=x[i][:].rearrange("r (t p) -> r t p", t=PACK),
+                    in0=centred[i][:].rearrange("r (p t) -> r t p", t=PACK),
+                    scalar=k[:, i : i + 1],
+                    in1=beta_bc[:].rearrange("r (p t) -> r t p", t=PACK),
+                    op0=ALU.mult, op1=ALU.add,
+                )
+                square_sum(x[i][:], x_sq[:, i : i + 1])
+
+        bias_sq = one_number("bias_sq")
+        bias_sq_clip = one_number("bias_sq_clip")
+        bias_norm = one_number("bias_norm")
+        bias_tanh = one_number("bias_tanh")
+        bias_rnorm = one_number("bias_rnorm")
+        y_scale = one_number("y_scale")
+        neg_y_scale = one_number("neg_y_scale")
+        y_sq = one_number("y_sq")
+        one_plus_y_sq = one_number("one_plus_y_sq")
+
+        def bias_square_sum():
+            square_sum(bias_bc[:], bias_sq[:])
+            load_table(ACT.Tanh, "warm_tanh_a")
+
+        def bias_norm_steps():
+            nc.vector.tensor_scalar_max(out=bias_sq_clip[:], in0=bias_sq[:], scalar1=NORM_MIN_SQ)
+            nc.gpsimd.tensor_tensor(
+                out=bias_norm[:], in0=bias_sq_clip[:], in1=half[:, 0:1], op=ALU.pow
+            )
+
+        def bias_tanh_step():
+            nc.scalar.activation(out=bias_tanh[:], in_=bias_norm[:], func=ACT.Tanh)
+
+        def bias_point_steps():
+            nc.vector.reciprocal(out=bias_rnorm[:], in_=bias_norm[:])
+            nc.vector.tensor_mul(out=y_scale[:], in0=bias_tanh[:], in1=bias_rnorm[:])
+            nc.vector.tensor_scalar_mul(out=neg_y_scale[:], in0=y_scale[:], scalar1=-1.0)
+            nc.vector.tensor_scalar(
+                out=y_sq[:], in0=bias_sq[:], scalar1=y_scale[:], scalar2=y_scale[:],
+                op0=ALU.mult, op1=ALU.mult,
+            )
+            nc.vector.tensor_scalar_add(out=one_plus_y_sq[:], in0=y_sq[:], scalar1=1.0)
+
+        w_grouped = keep.tile([P, D, PACK], BF16, name="w_grouped", align_bytes=64)
+        w_codes = keep.tile([P, D], U32, name="w_codes", align_bytes=64)
+        w_scales = keep.tile([P, D], U8, name="w_scales", align_bytes=64)
+        w_t = [psum_tr.tile([P, 2, PACK, P], BF16, name="w_t%d" % b, tag="tr") for b in range(2)]
+
+        def transpose_weight():
+            for b in range(2):
+                for a in range(2):
+                    for t in range(PACK):
+                        nc.tensor.transpose(
+                            out=w_t[b][:, a, t, :],
+                            in_=w_sb[:, 2 * b + a, t : D : PACK],
+                            identity=ident[:],
+                        )
+
+        def regroup_weight(b):
+            nc.scalar.copy(
+                out=w_grouped[:, 2 * b * P : 2 * (b + 1) * P, :].rearrange(
+                    "p (a r) t -> p a r t", a=2
+                ),
+                in_=w_t[b][:].rearrange("p a t r -> p a r t"),
+            )
+
+        def quantise_weight():
+            nc.vector.quantize_mx(
+                out=w_codes[:].bitcast(FP8X4),
+                scales=w_scales[:],
+                in_=w_grouped[:].rearrange("p c t -> p (c t)"),
+            )
+
+        shrink = row_numbers("shrink")
+        u = per_tile([P, D], BF16, "u")
+        u_t = {}
+        u_grouped = per_tile([P, P, PACK], BF16, "u_grouped")
+        u_codes = per_tile([P, P], U32, "u_codes")
+        u_scales = per_tile([P, P], U8, "u_scales")
+        xt = [psum_xt.tile([P, D], F32, name="xt%d" % i) for i in range(TILES)]
+        xt_sq = row_numbers("xt_sq")
+        xt_y = row_numbers("xt_y")
+        xt_norm = row_numbers("xt_norm")
+
+        def shrink_factor(rows):
+            c = cols(rows)
+            power(x_rnorm, x_sq, neg_half, rows)
+            nc.vector.tensor_scalar(
+                out=shrink[:, c], in0=x_rnorm[:, c], scalar1=ARTANH_BOUND, scalar2=1.0,
+                op0=ALU.mult, op1=ALU.min,
+            )
+
+        def make_u(rows):
+            for i in rows:
+                nc.vector.tensor_scalar_mul(out=u[i][:], in0=x[i][:], scalar1=shrink[:, i : i + 1])
+                u_t[i] = psum_tr.tile([P, PACK, P], BF16, name="u_t", tag="tr")
+                for t in range(PACK):
+                    nc.tensor.transpose(
+                        out=u_t[i][:, t, :], in_=u[i][:, t * P : (t + 1) * P], identity=ident[:]
+                    )
+
+        def regroup_u(rows):
+            for i in rows:
+                nc.scalar.copy(out=u_grouped[i][:], in_=u_t[i][:].rearrange("p t r -> p r t"))
+
+        def multiply(rows):
+            for i in rows:
+                nc.vector.quantize_mx(
+                    out=u_codes[i][:].bitcast(FP8X4),
+                    scales=u_scales[i][:],
+                    in_=u_grouped[i][:].rearrange("p r t -> p (r t)"),
+                )
+                nc.tensor.matmul_mx(
+                    out=xt[i][:],
+                    lhsT=u_codes[i][:].bitcast(FP8X4),
+                    lhsT_scale=u_scales[i][:],
+                    rhs=w_codes[:].bitcast(FP8X4),
+                    rhs_scale=w_scales[:],
+                    start=True,
+                    stop=True,
+                )
+
+        def row_sums(rows):
+            for i in rows:
+                square_sum(xt[i][:], xt_sq[:, i : i + 1])
+                products = scrap.tile([P, D], F32, name="products")
+                nc.vector.scalar_tensor_tensor(
+                    out=products[:], in0=xt[i][:], scalar=y_scale[:], in1=bias_bc[:],
+                    op0=ALU.mult, op1=ALU.mult, accum_out=xt_y[:, i : i + 1],
+                )
+
+        r_norm = row_numbers("r_norm")
+        xt_norm_clip = row_numbers("xt_norm_clip")
+        xt_rnorm = row_numbers("xt_rnorm")
+        xt_y_unit2 = row_numbers("xt_y_unit2")
+
+        def exp_map(rows):
+            c = cols(rows)
+            power(xt_norm, xt_sq, half, rows)
+            nc.scalar.activation(out=r_norm[:, c], in_=xt_norm[:, c], func=ACT.Tanh)
+            nc.vector.tensor_scalar_max(out=xt_norm_clip[:, c], in0=xt_norm[:, c], scalar1=NORM_MIN)
+            nc.vector.reciprocal(out=xt_rnorm[:, c], in_=xt_norm_clip[:, c])
+            nc.vector.scalar_tensor_tensor(
+                out=xt_y_unit2[:, c], in0=xt_rnorm[:, c], scalar=2.0, in1=xt_y[:, c],
+                op0=ALU.mult, op1=ALU.mult,
+            )
+
+        r_y2 = row_numbers("r_y2")
+        rho = row_numbers("rho")
+        r_sq = row_numbers("r_sq")
+        y_coef = row_numbers("y_coef")
+        xt_coef = row_numbers("xt_coef")
+        xt_rcoef = row_numbers("xt_rcoef")
+        bias_coef = row_numbers("bias_coef")
+        den_m1 = row_numbers("den_m1")
+        den = row_numbers("den")
+        sum_sq = row_numbers("sum_sq")
+        sum_den = row_numbers("sum_den")
+        sum_den_rsqrt = row_numbers("sum_den_rsqrt")
+        r2_norm = row_numbers("r2_norm")
+        r2_clip = row_numbers("r2_clip")
+
+        def moebius_coefficients(rows):
+            c = cols(rows)
+            nc.vector.tensor_mul(out=r_y2[:, c], in0=r_norm[:, c], in1=xt_y_unit2[:, c])
+            nc.vector.tensor_mul(out=rho[:, c], in0=r_norm[:, c], in1=xt_rnorm[:, c])
+            nc.vector.tensor_mul(out=r_sq[:, c], in0=r_norm[:, c], in1=r_norm[:, c])
+            nc.vector.scalar_tensor_tensor(
+                out=xt_coef[:, c], in0=r_y2[:, c], scalar=one_plus_y_sq[:], in1=rho[:, c],
+                op0=ALU.add, op1=ALU.mult,
+            )
+            nc.vector.tensor_scalar(
+                out=y_coef[:, c], in0=r_sq[:, c], scalar1=neg_y_scale[:], scalar2=y_scale[:],
+                op0=ALU.mult, op1=ALU.add,
+            )
+            nc.vector.scalar_tensor_tensor(
+                out=den_m1[:, c], in0=r_sq[:, c], scalar=y_sq[:], in1=r_y2[:, c],
+                op0=ALU.mult, op1=ALU.add,
+            )
+            nc.vector.reciprocal(out=xt_rcoef[:, c], in_=xt_coef[:, c])
+            nc.vector.scalar_tensor_tensor(
+                out=sum_sq[:, c], in0=r_sq[:, c], scalar=y_sq[:], in1=r_y2[:, c],
+                op0=ALU.add, op1=ALU.add,
+            )
+            nc.vector.tensor_scalar(
+                out=den[:, c], in0=den_m1[:, c], scalar1=1.0, scalar2=NORM_MIN,
+                op0=ALU.add, op1=ALU.max,
+            )
+            nc.vector.tensor_mul(out=bias_coef[:, c], in0=y_coef[:, c], in1=xt_rcoef[:, c])
+
+        def norm_of_r2(rows):
+            c = cols(rows)
+            nc.vector.scalar_tensor_tensor(
+                out=sum_den[:, c], in0=sum_sq[:, c], scalar=SUM_SQ_MIN, in1=den[:, c],
+                op0=ALU.max, op1=ALU.mult,
+            )
+            power(sum_den_rsqrt, sum_den, neg_half, rows)
+            nc.gpsimd.tensor_tensor(
+                out=r2_norm[:, c], in0=sum_sq[:, c], in1=sum_den_rsqrt[:, c], op=ALU.mult
+            )
+            nc.gpsimd.tensor_scalar_min(out=r2_clip[:, c], in0=r2_norm[:, c], scalar1=BOUND)
+
+        z = per_tile([P, D], F32, "z")
+        relu_sq = keep.tile([P, 2, 8], F32, name="relu_sq")
+        relu_norm = row_numbers("relu_norm")
+
+        def direction(rows):
+            for i in rows:
+                nc.vector.scalar_tensor_tensor(
+                    out=z[i][:], in0=bias_bc[:], scalar=bias_coef[:, i : i + 1], in1=xt[i][:],
+                    op0=ALU.mult, op1=ALU.add,
+                )
+
+        def relu_square_sums(rows):
+            for i in rows:
+                products = scrap.tile([P, D], F32, name="products")
+                nc.vector.scalar_tensor_tensor(
+                    out=products[:], in0=z[i][:], scalar=0.0, in1=z[i][:],
+                    op0=ALU.max, op1=ALU.mult, accum_out=relu_sq[:, i // 2, i % 2 : i % 2 + 1],
+                )
+
+        def relu_square_sums_on_scalar(rows):
+            for i in rows:
+                relu_z = scrap.tile([P, D], F32, name="relu_z")
+                nc.scalar.activation(out=relu_z[:], in_=z[i][:], func=ACT.Relu)
+                square_sum(relu_z[:], relu_sq[:, i // 2, i % 2 : i % 2 + 1])
+
+        ln_up2 = row_numbers("ln_up2")
+        ln_dn2 = row_numbers("ln_dn2")
+        z_unit = row_numbers("z_unit")
+        artanh2 = row_numbers("artanh2")
+        log_coef = row_numbers("log_coef")
+
+        def log_of_r2(rows):
+            c = cols(rows)
+            nc.scalar.activation(out=ln_up2[:, c], in_=r2_clip[:, c], func=ACT.Ln, bias=1.0, scale=1.0)
+            nc.scalar.activation(out=ln_dn2[:, c], in_=r2_clip[:, c], func=ACT.Ln, bias=1.0, scale=-1.0)
+
+        def log_map_coefficient(rows):
+            c = cols(rows)
+            nc.vector.tensor_mul(out=z_unit[:, c], in0=xt_coef[:, c], in1=sum_den_rsqrt[:, c])
+            nc.vector.tensor_sub(out=artanh2[:, c], in0=ln_up2[:, c], in1=ln_dn2[:, c])
+            nc.vector.scalar_tensor_tensor(
+                out=log_coef[:, c], in0=artanh2[:, c], scalar=0.5, in1=z_unit[:, c],
+                op0=ALU.mult, op1=ALU.mult,
+            )
+
+        v_norm = row_numbers("v_norm")
+        v_tanh = row_numbers("v_tanh")
+        relu_norm_clip = row_numbers("relu_norm_clip")
+        relu_rnorm = row_numbers("relu_rnorm")
+        out_coef = row_numbers("out_coef")
+        result = per_tile([P, D], F32, "result")
+
+        def out_coefficient(rows):
+            c = cols(rows)
+            nc.gpsimd.tensor_tensor(
+                out=relu_norm[:].rearrange("p (a b) -> p a b", a=2),
+                in0=relu_sq[:, :, 0:2],
+                in1=half[:].rearrange("p (a b) -> p a b", a=2),
+                op=ALU.pow,
+            )
+            nc.vector.scalar_tensor_tensor(
+                out=v_norm[:, c], in0=relu_norm[:, c], scalar=NORM_MIN, in1=log_coef[:, c],
+                op0=ALU.max, op1=ALU.mult,
+            )
+            nc.scalar.activation(out=v_tanh[:, c], in_=v_norm[:, c], func=ACT.Tanh)
+            nc.vector.tensor_scalar_max(out=relu_norm_clip[:, c], in0=relu_norm[:, c], scalar1=NORM_MIN)
+            nc.vector.reciprocal(out=relu_rnorm[:, c], in_=relu_norm_clip[:, c])
+            nc.vector.tensor_mul(out=out_coef[:, c], in0=v_tanh[:, c], in1=relu_rnorm[:, c])
+
+        def finish(rows):
+            for i in rows:
+                if i == TILES - 1:
+                    nc.scalar.activation(
+                        out=result[i][:], in_=z[i][:], func=ACT.Relu, scale=out_coef[:, i : i + 1]
+                    )
+                else:
+                    nc.vector.tensor_scalar(
+                        out=result[i][:], in0=z[i][:], scalar1=0.0, scalar2=out_coef[:, i : i + 1],
+                        op0=ALU.max, op1=ALU.mult,
+                    )
+                nc.sync.dma_start(out=out[i * P : (i + 1) * P, :], in_=result[i][:])
+
+        ALL = range(TILES)
+        PAIRS = [range(0, 2), range(2, 4)]
+        SINGLES = [range(i, i + 1) for i in range(TILES)]
+
+        transpose_weight()
+        shifted_sums(range(0, 3))
+        first_terms(ALL)
+        shifted_sums(range(3, 4))
+        norm_of_h(ALL)
+        regroup_weight(0)
+        centre(PAIRS[0])
+        variance(ALL)
+        log_of_h(ALL)
+        layer_norm_scale(ALL)
+        centre(PAIRS[1])
+        bias_square_sum()
+        bias_norm_steps()
+        bias_tanh_step()
+        layer_norm_factor(ALL)
+        layer_norm(ALL)
+        regroup_weight(1)
+        bias_point_steps()
+        for rows in PAIRS:
+            shrink_factor(rows)
+            make_u(rows)
+        quantise_weight()
+        regroup_u(ALL)
+        multiply(ALL)
+        row_sums(ALL)
+        exp_map(ALL)
+        moebius_coefficients(ALL)
+        load_table(ACT.Ln, "warm_ln_b")
+        direction(SINGLES[0])
+        norm_of_r2(ALL)
+        direction(range(1, 4))
+        relu_square_sums_on_scalar(PAIRS[0])
+        log_of_r2(ALL)
+        load_table(ACT.Tanh, "warm_tanh_b")
+        relu_square_sums(PAIRS[1])
+        log_map_coefficient(ALL)
+        out_coefficient(ALL)
+        finish(ALL)

@@ -64,20 +64,17 @@ def tile_hnnlayer_s_kernel(tc, h, weight, bias, gamma, beta, out):
             squares = scrap.tile([P, D], BF16, name="squares")
             nc.scalar.activation(out=squares[:], in_=src, func=ACT.Square, accum_out=total)
 
+        gamma_col = keep.tile([P, PACK], BF16, name="gamma_col")
+        beta_col = keep.tile([P, PACK], BF16, name="beta_col")
+        bias_col = keep.tile([P, PACK], BF16, name="bias_col")
+        nc.scalar.dma_start(out=gamma_col[:], in_=gamma.rearrange("(p t) -> p t", t=PACK))
+        nc.scalar.dma_start(out=beta_col[:], in_=beta.rearrange("(p t) -> p t", t=PACK))
+        nc.scalar.dma_start(out=bias_col[:], in_=bias.rearrange("o (p t) -> p (o t)", t=PACK))
         h_sb = keep.tile([P, TILES, D], BF16, name="h_sb")
         for i in range(TILES):
             nc.sync.dma_start(out=h_sb[:, i, :], in_=h[i * P : (i + 1) * P, :])
         w_sb = keep.tile([P, TILES, D], BF16, name="w_sb")
         nc.sync.dma_start(out=w_sb[:], in_=weight.rearrange("(o p) k -> p o k", p=P))
-        gamma_bc = keep.tile([P, D], BF16, name="gamma_bc")
-        nc.sync.dma_start(out=gamma_bc[:], in_=gamma.partition_broadcast(P))
-        bias_bc = keep.tile([P, D], BF16, name="bias_bc")
-        nc.sync.dma_start(
-            out=bias_bc[:], in_=bias.rearrange("o d -> (o d)").partition_broadcast(P)
-        )
-        beta_bc = keep.tile([P, D], BF16, name="beta_bc")
-        nc.sync.dma_start(out=beta_bc[:], in_=beta.partition_broadcast(P))
-
         half = row_numbers("half")
         nc.vector.memset(half[:], 0.5)
         neg_half = row_numbers("neg_half")
@@ -86,7 +83,29 @@ def tile_hnnlayer_s_kernel(tc, h, weight, bias, gamma, beta, out):
         nc.vector.memset(ones[:], 1.0)
         ident = keep.tile([P, P], BF16, name="ident")
         make_identity(nc, ident[:])
+        ident_words = keep.tile([P, P], F32, name="ident_words")
+        make_identity(nc, ident_words[:])
         load_table(ACT.Ln, "warm_ln_a")
+
+        gamma_bc = keep.tile([P, D], BF16, name="gamma_bc")
+        beta_bc = keep.tile([P, D], BF16, name="beta_bc")
+        bias_bc = keep.tile([P, D], BF16, name="bias_bc")
+        spread_ps = {}
+
+        def spread(vec_col, name):
+            spread_ps[name] = psum_tr.tile([P, PACK, P], BF16, name=name, tag="tr")
+            for t in range(PACK):
+                nc.tensor.transpose(
+                    out=spread_ps[name][:, t, :],
+                    in_=vec_col[:, t : t + 1].to_broadcast([P, P]),
+                    identity=ident[:],
+                )
+
+        def collect(dst, name):
+            nc.scalar.copy(
+                out=dst[:].rearrange("q (p t) -> q p t", t=PACK),
+                in_=spread_ps[name][:].rearrange("q t p -> q p t"),
+            )
 
         first = h_sb[:, :, 0]
         d = per_tile([P, D], F32, "d")
@@ -198,10 +217,7 @@ def tile_hnnlayer_s_kernel(tc, h, weight, bias, gamma, beta, out):
         def layer_norm(rows):
             for i in rows:
                 nc.vector.scalar_tensor_tensor(
-                    out=x[i][:].rearrange("r (t p) -> r t p", t=PACK),
-                    in0=centred[i][:].rearrange("r (p t) -> r t p", t=PACK),
-                    scalar=k[:, i : i + 1],
-                    in1=beta_bc[:].rearrange("r (p t) -> r t p", t=PACK),
+                    out=x[i][:], in0=centred[i][:], scalar=k[:, i : i + 1], in1=beta_bc[:],
                     op0=ALU.mult, op1=ALU.add,
                 )
                 square_sum(x[i][:], x_sq[:, i : i + 1])
@@ -242,24 +258,23 @@ def tile_hnnlayer_s_kernel(tc, h, weight, bias, gamma, beta, out):
         w_grouped = keep.tile([P, D, PACK], BF16, name="w_grouped", align_bytes=64)
         w_codes = keep.tile([P, D], U32, name="w_codes", align_bytes=64)
         w_scales = keep.tile([P, D], U8, name="w_scales", align_bytes=64)
-        w_t = [psum_tr.tile([P, 2, PACK, P], BF16, name="w_t%d" % b, tag="tr") for b in range(2)]
+        w_t = {}
 
-        def transpose_weight():
-            for b in range(2):
-                for a in range(2):
-                    for t in range(PACK):
-                        nc.tensor.transpose(
-                            out=w_t[b][:, a, t, :],
-                            in_=w_sb[:, 2 * b + a, t : D : PACK],
-                            identity=ident[:],
-                        )
+        def transpose_weight(b):
+            w_t[b] = psum_tr.tile([P, 2, 2, P], F32, name="w_t", tag="tr")
+            for a in range(2):
+                words = w_sb[:, 2 * b + a, :].bitcast(F32)
+                for v in range(2):
+                    nc.tensor.transpose(
+                        out=w_t[b][:, a, v, :], in_=words[:, v : D // 2 : 2], identity=ident_words[:]
+                    )
 
         def regroup_weight(b):
             nc.scalar.copy(
-                out=w_grouped[:, 2 * b * P : 2 * (b + 1) * P, :].rearrange(
-                    "p (a r) t -> p a r t", a=2
+                out=w_grouped[:, 2 * b * P : 2 * (b + 1) * P, :].bitcast(F32).rearrange(
+                    "p (a r) v -> p a r v", a=2
                 ),
-                in_=w_t[b][:].rearrange("p a t r -> p a r t"),
+                in_=w_t[b][:].rearrange("p a v r -> p a r v"),
             )
 
         def quantise_weight():
@@ -291,15 +306,18 @@ def tile_hnnlayer_s_kernel(tc, h, weight, bias, gamma, beta, out):
         def make_u(rows):
             for i in rows:
                 nc.vector.tensor_scalar_mul(out=u[i][:], in0=x[i][:], scalar1=shrink[:, i : i + 1])
-                u_t[i] = psum_tr.tile([P, PACK, P], BF16, name="u_t", tag="tr")
-                for t in range(PACK):
+                words = u[i][:].bitcast(F32)
+                u_t[i] = psum_tr.tile([P, 2, P], F32, name="u_t", tag="tr")
+                for v in range(2):
                     nc.tensor.transpose(
-                        out=u_t[i][:, t, :], in_=u[i][:, t * P : (t + 1) * P], identity=ident[:]
+                        out=u_t[i][:, v, :], in_=words[:, v : D // 2 : 2], identity=ident_words[:]
                     )
 
         def regroup_u(rows):
             for i in rows:
-                nc.scalar.copy(out=u_grouped[i][:], in_=u_t[i][:].rearrange("p t r -> p r t"))
+                nc.scalar.copy(
+                    out=u_grouped[i][:].bitcast(F32), in_=u_t[i][:].rearrange("p v r -> p r v")
+                )
 
         def multiply(rows):
             for i in rows:
@@ -484,17 +502,24 @@ def tile_hnnlayer_s_kernel(tc, h, weight, bias, gamma, beta, out):
         PAIRS = [range(0, 2), range(2, 4)]
         SINGLES = [range(i, i + 1) for i in range(TILES)]
 
-        transpose_weight()
+        spread(gamma_col, "gamma_ps")
+        transpose_weight(0)
+        transpose_weight(1)
         shifted_sums(range(0, 3))
         first_terms(ALL)
         shifted_sums(range(3, 4))
+        spread(beta_col, "beta_ps")
         norm_of_h(ALL)
+        collect(gamma_bc, "gamma_ps")
         regroup_weight(0)
+        spread(bias_col, "bias_ps")
+        collect(beta_bc, "beta_ps")
         centre(PAIRS[0])
         variance(ALL)
         log_of_h(ALL)
         layer_norm_scale(ALL)
         centre(PAIRS[1])
+        collect(bias_bc, "bias_ps")
         bias_square_sum()
         bias_norm_steps()
         bias_tanh_step()

@@ -33,8 +33,8 @@ def tile_hnnlayer_s_kernel(tc, h, weight, bias, gamma, beta, out):
     with ExitStack() as ctx:
         keep = ctx.enter_context(tc.tile_pool(name="keep", bufs=1))
         scrap = ctx.enter_context(tc.tile_pool(name="scrap", bufs=4))
-        psum_tr = ctx.enter_context(tc.psum_pool(name="psum_tr", bufs=4))
-        psum_xt = ctx.enter_context(tc.psum_pool(name="psum_xt", bufs=1))
+        psum_tr = ctx.enter_context(tc.psum_pool(name="psum_tr", bufs=3))
+        psum_keep = ctx.enter_context(tc.psum_pool(name="psum_keep", bufs=1))
         ctx.enter_context(tc.manual_schedule())
 
         def per_tile(shape, dtype, name):
@@ -52,13 +52,19 @@ def tile_hnnlayer_s_kernel(tc, h, weight, bias, gamma, beta, out):
         def cols(rows):
             return slice(rows[0], rows[-1] + 1)
 
+        def col(numbers, i):
+            return numbers[:, i : i + 1]
+
+        def by_four(features):
+            return features.rearrange("q (p t) -> q p t", t=PACK)
+
         def power(dst, src, exponent, rows):
             c = cols(rows)
             nc.gpsimd.tensor_tensor(out=dst[:, c], in0=src[:, c], in1=exponent[:, c], op=ALU.pow)
 
-        def load_table(func, name):
+        def load_table(func, name, source):
             unused = one_number(name)
-            nc.scalar.activation(out=unused[:], in_=ones[:], func=func)
+            nc.scalar.activation(out=unused[:], in_=source, func=func)
 
         def square_sum(src, total):
             squares = scrap.tile([P, D], BF16, name="squares")
@@ -68,8 +74,8 @@ def tile_hnnlayer_s_kernel(tc, h, weight, bias, gamma, beta, out):
         beta_col = keep.tile([P, PACK], BF16, name="beta_col")
         bias_col = keep.tile([P, PACK], BF16, name="bias_col")
         nc.scalar.dma_start(out=gamma_col[:], in_=gamma.rearrange("(p t) -> p t", t=PACK))
-        nc.scalar.dma_start(out=beta_col[:], in_=beta.rearrange("(p t) -> p t", t=PACK))
-        nc.scalar.dma_start(out=bias_col[:], in_=bias.rearrange("o (p t) -> p (o t)", t=PACK))
+        nc.gpsimd.dma_start(out=beta_col[:], in_=beta.rearrange("(p t) -> p t", t=PACK))
+        nc.gpsimd.dma_start(out=bias_col[:], in_=bias.rearrange("o (p t) -> p (o t)", t=PACK))
         h_sb = keep.tile([P, TILES, D], BF16, name="h_sb")
         for i in range(TILES):
             nc.sync.dma_start(out=h_sb[:, i, :], in_=h[i * P : (i + 1) * P, :])
@@ -85,53 +91,57 @@ def tile_hnnlayer_s_kernel(tc, h, weight, bias, gamma, beta, out):
         make_identity(nc, ident[:])
         ident_words = keep.tile([P, P], F32, name="ident_words")
         make_identity(nc, ident_words[:])
-        load_table(ACT.Ln, "warm_ln_a")
+        load_table(ACT.Ln, "warm_ln", ones[:])
 
-        gamma_bc = keep.tile([P, D], BF16, name="gamma_bc")
-        beta_bc = keep.tile([P, D], BF16, name="beta_bc")
+        affine_ps = psum_keep.tile([P, 2, PACK, P], BF16, name="affine_ps")
+        bias_ps = psum_tr.tile([P, PACK, P], BF16, name="bias_ps", tag="tr")
         bias_bc = keep.tile([P, D], BF16, name="bias_bc")
-        spread_ps = {}
+        gamma_bc = affine_ps[:, 0].rearrange("q t p -> q p t")
+        beta_bc = affine_ps[:, 1].rearrange("q t p -> q p t")
 
-        def spread(vec_col, name):
-            spread_ps[name] = psum_tr.tile([P, PACK, P], BF16, name=name, tag="tr")
+        def spread(vec_col, rows_ps):
             for t in range(PACK):
                 nc.tensor.transpose(
-                    out=spread_ps[name][:, t, :],
+                    out=rows_ps[:, t, :],
                     in_=vec_col[:, t : t + 1].to_broadcast([P, P]),
                     identity=ident[:],
                 )
 
-        def collect(dst, name):
+        def collect_bias():
             nc.scalar.copy(
-                out=dst[:].rearrange("q (p t) -> q p t", t=PACK),
-                in_=spread_ps[name][:].rearrange("q t p -> q p t"),
+                out=bias_bc[:].rearrange("q (p t) -> q p t", t=PACK),
+                in_=bias_ps[:].rearrange("q t p -> q p t"),
             )
 
         first = h_sb[:, :, 0]
-        d = per_tile([P, D], F32, "d")
         d_sum = row_numbers("d_sum")
         d_sq = row_numbers("d_sq")
 
-        def shifted_sums(rows):
-            for i in rows:
-                squares = scrap.tile([P, D], BF16, name="squares")
-                nc.scalar.activation(
-                    out=squares[:], in_=h_sb[:, i, :], func=ACT.Square, scale=-1.0,
-                    bias=h_sb[:, i, 0:1], accum_out=d_sq[:, i : i + 1],
-                )
-                nc.vector.tensor_scalar(
-                    out=d[i][:], in0=h_sb[:, i, :], scalar1=h_sb[:, i, 0:1], scalar2=None,
-                    op0=ALU.subtract, op1=ALU.add, accum_out=d_sum[:, i : i + 1],
-                )
+        def shifted_sum(i):
+            shifted = scrap.tile([P, D], F32, name="shifted")
+            nc.vector.tensor_scalar(
+                out=shifted[:], in0=h_sb[:, i, :], scalar1=h_sb[:, i, 0:1], scalar2=None,
+                op0=ALU.subtract, op1=ALU.add, accum_out=col(d_sum, i),
+            )
 
+        def shifted_square_sum(i):
+            squares = scrap.tile([P, D], BF16, name="squares")
+            nc.scalar.activation(
+                out=squares[:], in_=h_sb[:, i, :], func=ACT.Square, scale=-1.0,
+                bias=h_sb[:, i, 0:1], accum_out=col(d_sq, i),
+            )
+
+        mean = row_numbers("mean")
         first_x2 = row_numbers("first_x2")
         first_sq = row_numbers("first_sq")
         h_sq_a = row_numbers("h_sq_a")
         h_sq_b = row_numbers("h_sq_b")
+        neg_sum_sq = row_numbers("neg_sum_sq")
+        dev_sq = row_numbers("dev_sq")
         h_sq = row_numbers("h_sq")
-        h_norm = row_numbers("h_norm")
+        h_sq_clip = row_numbers("h_sq_clip")
         h_clip = row_numbers("h_clip")
-        d_mean = row_numbers("d_mean")
+        eps_h_sq = row_numbers("eps_h_sq")
 
         def first_terms(rows):
             c = cols(rows)
@@ -143,114 +153,131 @@ def tile_hnnlayer_s_kernel(tc, h, weight, bias, gamma, beta, out):
 
         def norm_of_h(rows):
             c = cols(rows)
-            nc.vector.tensor_add(out=h_sq_a[:, c], in0=d_sq[:, c], in1=first_sq[:, c])
-            nc.vector.tensor_mul(out=h_sq_b[:, c], in0=d_sum[:, c], in1=first_x2[:, c])
-            nc.vector.tensor_add(out=h_sq[:, c], in0=h_sq_a[:, c], in1=h_sq_b[:, c])
-            power(h_norm, h_sq, half, rows)
-            nc.gpsimd.tensor_scalar_min(out=h_clip[:, c], in0=h_norm[:, c], scalar1=BOUND)
-            nc.vector.tensor_scalar_mul(out=d_mean[:, c], in0=d_sum[:, c], scalar1=1.0 / D)
+            nc.vector.tensor_mul(out=h_sq_a[:, c], in0=d_sum[:, c], in1=first_x2[:, c])
+            nc.vector.scalar_tensor_tensor(
+                out=mean[:, c], in0=d_sum[:, c], scalar=1.0 / D, in1=first[:, c],
+                op0=ALU.mult, op1=ALU.add,
+            )
+            nc.vector.scalar_tensor_tensor(
+                out=neg_sum_sq[:, c], in0=d_sum[:, c], scalar=-1.0 / D, in1=d_sum[:, c],
+                op0=ALU.mult, op1=ALU.mult,
+            )
+            nc.vector.tensor_add(out=h_sq_b[:, c], in0=h_sq_a[:, c], in1=first_sq[:, c])
+            nc.vector.tensor_add(out=h_sq[:, c], in0=h_sq_b[:, c], in1=d_sq[:, c])
+            nc.vector.tensor_add(out=dev_sq[:, c], in0=neg_sum_sq[:, c], in1=d_sq[:, c])
+            nc.vector.tensor_scalar_min(out=h_sq_clip[:, c], in0=h_sq[:, c], scalar1=BOUND * BOUND)
+
+        def root_of_h(rows):
+            power(h_clip, h_sq_clip, half, rows)
+
+        def eps_of_h(rows):
+            c = cols(rows)
+            nc.gpsimd.tensor_scalar(
+                out=eps_h_sq[:, c], in0=h_sq[:, c], scalar1=NORM_MIN_SQ, scalar2=4.0 * D * LN_EPS,
+                op0=ALU.max, op1=ALU.mult,
+            )
 
         centred = per_tile([P, D], F32, "centred")
 
-        def centre(rows):
-            for i in rows:
-                nc.vector.scalar_tensor_tensor(
-                    out=centred[i][:], in0=d[i][:], scalar=d_mean[:, i : i + 1],
-                    in1=gamma_bc[:], op0=ALU.subtract, op1=ALU.mult,
-                )
-
-        d_sum_mean = row_numbers("d_sum_mean")
-        dev_sq = row_numbers("dev_sq")
-        eps_h_sq = row_numbers("eps_h_sq")
-        quarter_var = row_numbers("quarter_var")
-
-        def variance(rows):
-            c = cols(rows)
-            nc.vector.tensor_mul(out=d_sum_mean[:, c], in0=d_sum[:, c], in1=d_mean[:, c])
-            nc.vector.tensor_sub(out=dev_sq[:, c], in0=d_sq[:, c], in1=d_sum_mean[:, c])
-            nc.vector.tensor_scalar(
-                out=eps_h_sq[:, c], in0=h_sq[:, c], scalar1=NORM_MIN_SQ, scalar2=LN_EPS,
-                op0=ALU.max, op1=ALU.mult,
+        def centre(i):
+            nc.vector.scalar_tensor_tensor(
+                out=by_four(centred[i][:]), in0=by_four(h_sb[:, i, :]), scalar=col(mean, i),
+                in1=gamma_bc, op0=ALU.subtract, op1=ALU.mult,
             )
-            nc.vector.tensor_scalar_mul(out=quarter_var[:, c], in0=dev_sq[:, c], scalar1=0.25 / D)
 
         ln_up = row_numbers("ln_up")
         ln_dn = row_numbers("ln_dn")
+        theta_sq = row_numbers("theta_sq")
+        theta2 = row_numbers("theta2")
+        k_arg = row_numbers("k_arg")
+        k_rsqrt = row_numbers("k_rsqrt")
+        k = row_numbers("k")
 
         def log_of_h(rows):
             c = cols(rows)
             nc.scalar.activation(out=ln_up[:, c], in_=h_clip[:, c], func=ACT.Ln, bias=1.0, scale=1.0)
             nc.scalar.activation(out=ln_dn[:, c], in_=h_clip[:, c], func=ACT.Ln, bias=1.0, scale=-1.0)
-
-        theta2 = row_numbers("theta2")
-        theta_sq = row_numbers("theta_sq")
-        k_arg = row_numbers("k_arg")
-        k_rsqrt = row_numbers("k_rsqrt")
-        k = row_numbers("k")
-
-        def layer_norm_scale(rows):
-            c = cols(rows)
             for i in rows:
                 nc.scalar.activation(
-                    out=theta_sq[:, i : i + 1], in_=ln_dn[:, i : i + 1], func=ACT.Square,
-                    scale=-1.0, bias=ln_up[:, i : i + 1],
+                    out=col(theta_sq, i), in_=col(ln_dn, i), func=ACT.Square,
+                    scale=-1.0, bias=col(ln_up, i),
                 )
             for i in rows:
                 nc.scalar.activation(
-                    out=k_arg[:, i : i + 1], in_=theta_sq[:, i : i + 1], func=ACT.Identity,
-                    scale=quarter_var[:, i : i + 1], bias=eps_h_sq[:, i : i + 1],
+                    out=col(k_arg, i), in_=col(theta_sq, i), func=ACT.Identity,
+                    scale=col(dev_sq, i), bias=col(eps_h_sq, i),
                 )
+
+        def root_of_k(rows):
             power(k_rsqrt, k_arg, neg_half, rows)
+
+        def layer_norm_factor(rows):
+            c = cols(rows)
             nc.vector.tensor_sub(out=theta2[:, c], in0=ln_up[:, c], in1=ln_dn[:, c])
+            nc.vector.scalar_tensor_tensor(
+                out=k[:, c], in0=theta2[:, c], scalar=math.sqrt(D), in1=k_rsqrt[:, c],
+                op0=ALU.mult, op1=ALU.mult,
+            )
 
         x = per_tile([P, D], F32, "x")
         x_sq = row_numbers("x_sq")
         x_rnorm = row_numbers("x_rnorm")
 
-        def layer_norm_factor(rows):
-            c = cols(rows)
+        def layer_norm(i):
             nc.vector.scalar_tensor_tensor(
-                out=k[:, c], in0=theta2[:, c], scalar=0.5, in1=k_rsqrt[:, c],
-                op0=ALU.mult, op1=ALU.mult,
+                out=by_four(x[i][:]), in0=by_four(centred[i][:]), scalar=col(k, i), in1=beta_bc,
+                op0=ALU.mult, op1=ALU.add,
             )
 
-        def layer_norm(rows):
-            for i in rows:
-                nc.vector.scalar_tensor_tensor(
-                    out=x[i][:], in0=centred[i][:], scalar=k[:, i : i + 1], in1=beta_bc[:],
-                    op0=ALU.mult, op1=ALU.add,
-                )
-                square_sum(x[i][:], x_sq[:, i : i + 1])
+        def square_sum_of_x(i):
+            square_sum(x[i][:], col(x_sq, i))
+
+        def square_sum_of_x_on_vector(i):
+            products = scrap.tile([P, D], F32, name="products")
+            nc.vector.scalar_tensor_tensor(
+                out=products[:], in0=x[i][:], scalar=1.0, in1=x[i][:],
+                op0=ALU.mult, op1=ALU.mult, accum_out=col(x_sq, i),
+            )
 
         bias_sq = one_number("bias_sq")
         bias_sq_clip = one_number("bias_sq_clip")
         bias_norm = one_number("bias_norm")
-        bias_tanh = one_number("bias_tanh")
         bias_rnorm = one_number("bias_rnorm")
+        y_norm = one_number("y_norm")
         y_scale = one_number("y_scale")
+        y_scale2 = one_number("y_scale2")
         neg_y_scale = one_number("neg_y_scale")
         y_sq = one_number("y_sq")
         one_plus_y_sq = one_number("one_plus_y_sq")
 
         def bias_square_sum():
-            square_sum(bias_bc[:], bias_sq[:])
-            load_table(ACT.Tanh, "warm_tanh_a")
+            products = scrap.tile([P, D], F32, name="products")
+            nc.vector.scalar_tensor_tensor(
+                out=products[:], in0=bias_bc[:], scalar=1.0, in1=bias_bc[:],
+                op0=ALU.mult, op1=ALU.mult, accum_out=bias_sq[:],
+            )
 
         def bias_norm_steps():
-            nc.vector.tensor_scalar_max(out=bias_sq_clip[:], in0=bias_sq[:], scalar1=NORM_MIN_SQ)
+            nc.gpsimd.tensor_scalar_max(out=bias_sq_clip[:], in0=bias_sq[:], scalar1=NORM_MIN_SQ)
             nc.gpsimd.tensor_tensor(
                 out=bias_norm[:], in0=bias_sq_clip[:], in1=half[:, 0:1], op=ALU.pow
             )
 
         def bias_tanh_step():
-            nc.scalar.activation(out=bias_tanh[:], in_=bias_norm[:], func=ACT.Tanh)
+            nc.scalar.activation(out=y_norm[:], in_=bias_norm[:], func=ACT.Tanh)
 
-        def bias_point_steps():
+        def bias_point_1():
             nc.vector.reciprocal(out=bias_rnorm[:], in_=bias_norm[:])
-            nc.vector.tensor_mul(out=y_scale[:], in0=bias_tanh[:], in1=bias_rnorm[:])
-            nc.vector.tensor_scalar_mul(out=neg_y_scale[:], in0=y_scale[:], scalar1=-1.0)
+            nc.vector.tensor_mul(out=y_sq[:], in0=y_norm[:], in1=y_norm[:])
+
+        def bias_point_2():
+            nc.vector.tensor_mul(out=y_scale[:], in0=y_norm[:], in1=bias_rnorm[:])
             nc.vector.tensor_scalar(
-                out=y_sq[:], in0=bias_sq[:], scalar1=y_scale[:], scalar2=y_scale[:],
+                out=y_scale2[:], in0=y_norm[:], scalar1=bias_rnorm[:], scalar2=2.0,
+                op0=ALU.mult, op1=ALU.mult,
+            )
+            nc.vector.tensor_scalar(
+                out=neg_y_scale[:], in0=y_norm[:], scalar1=bias_rnorm[:], scalar2=-1.0,
                 op0=ALU.mult, op1=ALU.mult,
             )
             nc.vector.tensor_scalar_add(out=one_plus_y_sq[:], in0=y_sq[:], scalar1=1.0)
@@ -290,76 +317,72 @@ def tile_hnnlayer_s_kernel(tc, h, weight, bias, gamma, beta, out):
         u_grouped = per_tile([P, P, PACK], BF16, "u_grouped")
         u_codes = per_tile([P, P], U32, "u_codes")
         u_scales = per_tile([P, P], U8, "u_scales")
-        xt = [psum_xt.tile([P, D], F32, name="xt%d" % i) for i in range(TILES)]
+        xt = [psum_keep.tile([P, D], F32, name="xt%d" % i) for i in range(TILES)]
         xt_sq = row_numbers("xt_sq")
-        xt_y = row_numbers("xt_y")
-        xt_norm = row_numbers("xt_norm")
+        xt_y2 = row_numbers("xt_y2")
+
+        def norm_of_x(rows):
+            power(x_rnorm, x_sq, neg_half, rows)
 
         def shrink_factor(rows):
             c = cols(rows)
-            power(x_rnorm, x_sq, neg_half, rows)
             nc.vector.tensor_scalar(
                 out=shrink[:, c], in0=x_rnorm[:, c], scalar1=ARTANH_BOUND, scalar2=1.0,
                 op0=ALU.mult, op1=ALU.min,
             )
 
-        def make_u(rows):
-            for i in rows:
-                nc.vector.tensor_scalar_mul(out=u[i][:], in0=x[i][:], scalar1=shrink[:, i : i + 1])
-                words = u[i][:].bitcast(F32)
-                u_t[i] = psum_tr.tile([P, 2, P], F32, name="u_t", tag="tr")
-                for v in range(2):
-                    nc.tensor.transpose(
-                        out=u_t[i][:, v, :], in_=words[:, v : D // 2 : 2], identity=ident_words[:]
-                    )
-
-        def regroup_u(rows):
-            for i in rows:
-                nc.scalar.copy(
-                    out=u_grouped[i][:].bitcast(F32), in_=u_t[i][:].rearrange("p v r -> p r v")
+        def make_u(i):
+            nc.vector.tensor_scalar_mul(out=u[i][:], in0=x[i][:], scalar1=col(shrink, i))
+            words = u[i][:].bitcast(F32)
+            if i % 2 == 0:
+                u_t[i // 2] = psum_tr.tile([P, 2, 2, P], F32, name="u_t", tag="tr")
+            for v in range(2):
+                nc.tensor.transpose(
+                    out=u_t[i // 2][:, i % 2, v, :], in_=words[:, v : D // 2 : 2], identity=ident_words[:]
                 )
 
-        def multiply(rows):
-            for i in rows:
-                nc.vector.quantize_mx(
-                    out=u_codes[i][:].bitcast(FP8X4),
-                    scales=u_scales[i][:],
-                    in_=u_grouped[i][:].rearrange("p r t -> p (r t)"),
-                )
-                nc.tensor.matmul_mx(
-                    out=xt[i][:],
-                    lhsT=u_codes[i][:].bitcast(FP8X4),
-                    lhsT_scale=u_scales[i][:],
-                    rhs=w_codes[:].bitcast(FP8X4),
-                    rhs_scale=w_scales[:],
-                    start=True,
-                    stop=True,
-                )
-
-        def row_sums(rows):
-            for i in rows:
-                square_sum(xt[i][:], xt_sq[:, i : i + 1])
-                products = scrap.tile([P, D], F32, name="products")
-                nc.vector.scalar_tensor_tensor(
-                    out=products[:], in0=xt[i][:], scalar=y_scale[:], in1=bias_bc[:],
-                    op0=ALU.mult, op1=ALU.mult, accum_out=xt_y[:, i : i + 1],
-                )
-
-        r_norm = row_numbers("r_norm")
-        xt_norm_clip = row_numbers("xt_norm_clip")
-        xt_rnorm = row_numbers("xt_rnorm")
-        xt_y_unit2 = row_numbers("xt_y_unit2")
-
-        def exp_map(rows):
-            c = cols(rows)
-            power(xt_norm, xt_sq, half, rows)
-            nc.scalar.activation(out=r_norm[:, c], in_=xt_norm[:, c], func=ACT.Tanh)
-            nc.vector.tensor_scalar_max(out=xt_norm_clip[:, c], in0=xt_norm[:, c], scalar1=NORM_MIN)
-            nc.vector.reciprocal(out=xt_rnorm[:, c], in_=xt_norm_clip[:, c])
-            nc.vector.scalar_tensor_tensor(
-                out=xt_y_unit2[:, c], in0=xt_rnorm[:, c], scalar=2.0, in1=xt_y[:, c],
-                op0=ALU.mult, op1=ALU.mult,
+        def regroup_u(i):
+            nc.scalar.copy(
+                out=u_grouped[i][:].bitcast(F32), in_=u_t[i // 2][:, i % 2].rearrange("p v r -> p r v")
             )
+
+        def multiply(i):
+            nc.vector.quantize_mx(
+                out=u_codes[i][:].bitcast(FP8X4),
+                scales=u_scales[i][:],
+                in_=u_grouped[i][:].rearrange("p r t -> p (r t)"),
+            )
+            nc.tensor.matmul_mx(
+                out=xt[i][:],
+                lhsT=u_codes[i][:].bitcast(FP8X4),
+                lhsT_scale=u_scales[i][:],
+                rhs=w_codes[:].bitcast(FP8X4),
+                rhs_scale=w_scales[:],
+                start=True,
+                stop=True,
+            )
+
+        def square_sum_of_xt(i):
+            square_sum(xt[i][:], col(xt_sq, i))
+
+        def dot_with_y(i):
+            products = scrap.tile([P, D], F32, name="products")
+            nc.vector.scalar_tensor_tensor(
+                out=products[:], in0=xt[i][:], scalar=y_scale2[:], in1=bias_bc[:],
+                op0=ALU.mult, op1=ALU.mult, accum_out=col(xt_y2, i),
+            )
+
+        xt_norm = row_numbers("xt_norm")
+        xt_norm_clip = row_numbers("xt_norm_clip")
+        r_norm = row_numbers("r_norm")
+        xt_rnorm = row_numbers("xt_rnorm")
+
+        def norm_of_xt(rows):
+            power(xt_norm, xt_sq, half, rows)
+
+        def tanh_of_norm(rows):
+            c = cols(rows)
+            nc.scalar.activation(out=r_norm[:, c], in_=xt_norm[:, c], func=ACT.Tanh)
 
         r_y2 = row_numbers("r_y2")
         rho = row_numbers("rho")
@@ -375,91 +398,113 @@ def tile_hnnlayer_s_kernel(tc, h, weight, bias, gamma, beta, out):
         sum_den_rsqrt = row_numbers("sum_den_rsqrt")
         r2_norm = row_numbers("r2_norm")
         r2_clip = row_numbers("r2_clip")
+        z_unit = row_numbers("z_unit")
+        ln_up2 = row_numbers("ln_up2")
+        ln_dn2 = row_numbers("ln_dn2")
+        artanh2 = row_numbers("artanh2")
+        log_coef = row_numbers("log_coef")
 
-        def moebius_coefficients(rows):
+        def moebius_1(rows):
             c = cols(rows)
-            nc.vector.tensor_mul(out=r_y2[:, c], in0=r_norm[:, c], in1=xt_y_unit2[:, c])
+            nc.vector.tensor_scalar_max(out=xt_norm_clip[:, c], in0=xt_norm[:, c], scalar1=NORM_MIN)
+
+        def moebius_2(rows):
+            c = cols(rows)
+            nc.vector.reciprocal(out=xt_rnorm[:, c], in_=xt_norm_clip[:, c])
+
+        def moebius_3(rows):
+            c = cols(rows)
             nc.vector.tensor_mul(out=rho[:, c], in0=r_norm[:, c], in1=xt_rnorm[:, c])
             nc.vector.tensor_mul(out=r_sq[:, c], in0=r_norm[:, c], in1=r_norm[:, c])
-            nc.vector.scalar_tensor_tensor(
-                out=xt_coef[:, c], in0=r_y2[:, c], scalar=one_plus_y_sq[:], in1=rho[:, c],
-                op0=ALU.add, op1=ALU.mult,
-            )
+
+        def moebius_4(rows):
+            c = cols(rows)
+            nc.vector.tensor_mul(out=r_y2[:, c], in0=rho[:, c], in1=xt_y2[:, c])
             nc.vector.tensor_scalar(
                 out=y_coef[:, c], in0=r_sq[:, c], scalar1=neg_y_scale[:], scalar2=y_scale[:],
                 op0=ALU.mult, op1=ALU.add,
+            )
+
+        def moebius_5(rows):
+            c = cols(rows)
+            nc.vector.scalar_tensor_tensor(
+                out=xt_coef[:, c], in0=r_y2[:, c], scalar=one_plus_y_sq[:], in1=rho[:, c],
+                op0=ALU.add, op1=ALU.mult,
             )
             nc.vector.scalar_tensor_tensor(
                 out=den_m1[:, c], in0=r_sq[:, c], scalar=y_sq[:], in1=r_y2[:, c],
                 op0=ALU.mult, op1=ALU.add,
             )
-            nc.vector.reciprocal(out=xt_rcoef[:, c], in_=xt_coef[:, c])
             nc.vector.scalar_tensor_tensor(
                 out=sum_sq[:, c], in0=r_sq[:, c], scalar=y_sq[:], in1=r_y2[:, c],
                 op0=ALU.add, op1=ALU.add,
             )
+
+        def moebius_6(rows):
+            c = cols(rows)
+            nc.vector.reciprocal(out=xt_rcoef[:, c], in_=xt_coef[:, c])
             nc.vector.tensor_scalar(
                 out=den[:, c], in0=den_m1[:, c], scalar1=1.0, scalar2=NORM_MIN,
                 op0=ALU.add, op1=ALU.max,
             )
-            nc.vector.tensor_mul(out=bias_coef[:, c], in0=y_coef[:, c], in1=xt_rcoef[:, c])
 
-        def norm_of_r2(rows):
+        def moebius_7(rows):
             c = cols(rows)
+            nc.vector.tensor_mul(out=bias_coef[:, c], in0=y_coef[:, c], in1=xt_rcoef[:, c])
             nc.vector.scalar_tensor_tensor(
                 out=sum_den[:, c], in0=sum_sq[:, c], scalar=SUM_SQ_MIN, in1=den[:, c],
                 op0=ALU.max, op1=ALU.mult,
             )
+
+        def root_of_r2(rows):
             power(sum_den_rsqrt, sum_den, neg_half, rows)
-            nc.gpsimd.tensor_tensor(
-                out=r2_norm[:, c], in0=sum_sq[:, c], in1=sum_den_rsqrt[:, c], op=ALU.mult
-            )
-            nc.gpsimd.tensor_scalar_min(out=r2_clip[:, c], in0=r2_norm[:, c], scalar1=BOUND)
 
-        z = per_tile([P, D], F32, "z")
-        relu_sq = keep.tile([P, 2, 8], F32, name="relu_sq")
-        relu_norm = row_numbers("relu_norm")
+        def norm_and_unit_of_r2(rows):
+            c = cols(rows)
+            nc.vector.tensor_mul(out=r2_norm[:, c], in0=sum_sq[:, c], in1=sum_den_rsqrt[:, c])
+            nc.vector.tensor_mul(out=z_unit[:, c], in0=xt_coef[:, c], in1=sum_den_rsqrt[:, c])
 
-        def direction(rows):
-            for i in rows:
-                nc.vector.scalar_tensor_tensor(
-                    out=z[i][:], in0=bias_bc[:], scalar=bias_coef[:, i : i + 1], in1=xt[i][:],
-                    op0=ALU.mult, op1=ALU.add,
-                )
-
-        def relu_square_sums(rows):
-            for i in rows:
-                products = scrap.tile([P, D], F32, name="products")
-                nc.vector.scalar_tensor_tensor(
-                    out=products[:], in0=z[i][:], scalar=0.0, in1=z[i][:],
-                    op0=ALU.max, op1=ALU.mult, accum_out=relu_sq[:, i // 2, i % 2 : i % 2 + 1],
-                )
-
-        def relu_square_sums_on_scalar(rows):
-            for i in rows:
-                relu_z = scrap.tile([P, D], F32, name="relu_z")
-                nc.scalar.activation(out=relu_z[:], in_=z[i][:], func=ACT.Relu)
-                square_sum(relu_z[:], relu_sq[:, i // 2, i % 2 : i % 2 + 1])
-
-        ln_up2 = row_numbers("ln_up2")
-        ln_dn2 = row_numbers("ln_dn2")
-        z_unit = row_numbers("z_unit")
-        artanh2 = row_numbers("artanh2")
-        log_coef = row_numbers("log_coef")
+        def clip_of_r2(rows):
+            c = cols(rows)
+            nc.vector.tensor_scalar_min(out=r2_clip[:, c], in0=r2_norm[:, c], scalar1=BOUND)
 
         def log_of_r2(rows):
             c = cols(rows)
             nc.scalar.activation(out=ln_up2[:, c], in_=r2_clip[:, c], func=ACT.Ln, bias=1.0, scale=1.0)
             nc.scalar.activation(out=ln_dn2[:, c], in_=r2_clip[:, c], func=ACT.Ln, bias=1.0, scale=-1.0)
 
+        def artanh_of_r2(rows):
+            c = cols(rows)
+            nc.vector.tensor_sub(out=artanh2[:, c], in0=ln_up2[:, c], in1=ln_dn2[:, c])
+
         def log_map_coefficient(rows):
             c = cols(rows)
-            nc.vector.tensor_mul(out=z_unit[:, c], in0=xt_coef[:, c], in1=sum_den_rsqrt[:, c])
-            nc.vector.tensor_sub(out=artanh2[:, c], in0=ln_up2[:, c], in1=ln_dn2[:, c])
             nc.vector.scalar_tensor_tensor(
                 out=log_coef[:, c], in0=artanh2[:, c], scalar=0.5, in1=z_unit[:, c],
                 op0=ALU.mult, op1=ALU.mult,
             )
+
+        z = per_tile([P, D], F32, "z")
+        relu_sq = row_numbers("relu_sq")
+        relu_norm = row_numbers("relu_norm")
+
+        def direction(i):
+            nc.vector.scalar_tensor_tensor(
+                out=z[i][:], in0=bias_bc[:], scalar=col(bias_coef, i), in1=xt[i][:],
+                op0=ALU.mult, op1=ALU.add,
+            )
+
+        def relu_square_sum(i):
+            products = scrap.tile([P, D], F32, name="products")
+            nc.vector.scalar_tensor_tensor(
+                out=products[:], in0=z[i][:], scalar=0.0, in1=z[i][:],
+                op0=ALU.max, op1=ALU.mult, accum_out=col(relu_sq, i),
+            )
+
+        def relu_square_sum_on_scalar(i):
+            relu_z = scrap.tile([P, D], F32, name="relu_z")
+            nc.scalar.activation(out=relu_z[:], in_=z[i][:], func=ACT.Relu)
+            square_sum(relu_z[:], col(relu_sq, i))
 
         v_norm = row_numbers("v_norm")
         v_tanh = row_numbers("v_tanh")
@@ -468,82 +513,154 @@ def tile_hnnlayer_s_kernel(tc, h, weight, bias, gamma, beta, out):
         out_coef = row_numbers("out_coef")
         result = per_tile([P, D], F32, "result")
 
-        def out_coefficient(rows):
+        def norm_of_relu(rows):
+            power(relu_norm, relu_sq, half, rows)
+
+        def norm_of_v(rows):
             c = cols(rows)
-            nc.gpsimd.tensor_tensor(
-                out=relu_norm[:].rearrange("p (a b) -> p a b", a=2),
-                in0=relu_sq[:, :, 0:2],
-                in1=half[:].rearrange("p (a b) -> p a b", a=2),
-                op=ALU.pow,
-            )
             nc.vector.scalar_tensor_tensor(
                 out=v_norm[:, c], in0=relu_norm[:, c], scalar=NORM_MIN, in1=log_coef[:, c],
                 op0=ALU.max, op1=ALU.mult,
             )
+            nc.vector.tensor_scalar_max(
+                out=relu_norm_clip[:, c], in0=relu_norm[:, c], scalar1=NORM_MIN
+            )
+
+        def tanh_of_v(rows):
+            c = cols(rows)
             nc.scalar.activation(out=v_tanh[:, c], in_=v_norm[:, c], func=ACT.Tanh)
-            nc.vector.tensor_scalar_max(out=relu_norm_clip[:, c], in0=relu_norm[:, c], scalar1=NORM_MIN)
+
+        def reciprocal_of_relu(rows):
+            c = cols(rows)
             nc.vector.reciprocal(out=relu_rnorm[:, c], in_=relu_norm_clip[:, c])
+
+        def out_coefficient(rows):
+            c = cols(rows)
             nc.vector.tensor_mul(out=out_coef[:, c], in0=v_tanh[:, c], in1=relu_rnorm[:, c])
 
-        def finish(rows):
-            for i in rows:
-                if i == TILES - 1:
-                    nc.scalar.activation(
-                        out=result[i][:], in_=z[i][:], func=ACT.Relu, scale=out_coef[:, i : i + 1]
-                    )
-                else:
-                    nc.vector.tensor_scalar(
-                        out=result[i][:], in0=z[i][:], scalar1=0.0, scalar2=out_coef[:, i : i + 1],
-                        op0=ALU.max, op1=ALU.mult,
-                    )
-                nc.sync.dma_start(out=out[i * P : (i + 1) * P, :], in_=result[i][:])
+        def store(i):
+            nc.sync.dma_start(out=out[i * P : (i + 1) * P, :], in_=result[i][:])
+
+        def finish_on_scalar(i):
+            nc.scalar.activation(out=result[i][:], in_=z[i][:], func=ACT.Relu, scale=col(out_coef, i))
+            store(i)
+
+        def finish(i):
+            nc.vector.tensor_scalar(
+                out=result[i][:], in0=z[i][:], scalar1=0.0, scalar2=col(out_coef, i),
+                op0=ALU.max, op1=ALU.mult,
+            )
+            store(i)
 
         ALL = range(TILES)
-        PAIRS = [range(0, 2), range(2, 4)]
-        SINGLES = [range(i, i + 1) for i in range(TILES)]
+        A = range(0, 2)
+        B = range(2, 4)
 
-        spread(gamma_col, "gamma_ps")
+        spread(gamma_col, affine_ps[:, 0])
+        shifted_square_sum(0)
+        shifted_sum(0)
+        shifted_square_sum(1)
+        shifted_sum(1)
+        shifted_square_sum(2)
+        shifted_sum(2)
+        first_terms(ALL)
+        shifted_square_sum(3)
+        shifted_sum(3)
+        spread(bias_col, bias_ps)
+        spread(beta_col, affine_ps[:, 1])
+        collect_bias()
         transpose_weight(0)
         transpose_weight(1)
-        shifted_sums(range(0, 3))
-        first_terms(ALL)
-        shifted_sums(range(3, 4))
-        spread(beta_col, "beta_ps")
         norm_of_h(ALL)
-        collect(gamma_bc, "gamma_ps")
+        root_of_h(ALL)
+        eps_of_h(ALL)
+        centre(0)
+        centre(1)
         regroup_weight(0)
-        spread(bias_col, "bias_ps")
-        collect(beta_bc, "beta_ps")
-        centre(PAIRS[0])
-        variance(ALL)
+        regroup_weight(1)
         log_of_h(ALL)
-        layer_norm_scale(ALL)
-        centre(PAIRS[1])
-        collect(bias_bc, "bias_ps")
+        load_table(ACT.Tanh, "warm_tanh_a", col(k_arg, 3))
+        root_of_k(A)
+        root_of_k(B)
+        centre(2)
+        centre(3)
         bias_square_sum()
         bias_norm_steps()
+        layer_norm_factor(A)
+        layer_norm(0)
+        layer_norm(1)
+        square_sum_of_x(0)
+        square_sum_of_x(1)
         bias_tanh_step()
-        layer_norm_factor(ALL)
-        layer_norm(ALL)
-        regroup_weight(1)
-        bias_point_steps()
-        for rows in PAIRS:
-            shrink_factor(rows)
-            make_u(rows)
+        norm_of_x(A)
+        layer_norm_factor(B)
+        layer_norm(2)
+        layer_norm(3)
+        square_sum_of_x(2)
+        square_sum_of_x(3)
+        norm_of_x(B)
         quantise_weight()
-        regroup_u(ALL)
-        multiply(ALL)
-        row_sums(ALL)
-        exp_map(ALL)
-        moebius_coefficients(ALL)
-        load_table(ACT.Ln, "warm_ln_b")
-        direction(SINGLES[0])
-        norm_of_r2(ALL)
-        direction(range(1, 4))
-        relu_square_sums_on_scalar(PAIRS[0])
+        shrink_factor(A)
+        bias_point_1()
+        make_u(0)
+        make_u(1)
+        bias_point_2()
+        regroup_u(0)
+        regroup_u(1)
+        shrink_factor(B)
+        make_u(2)
+        make_u(3)
+        multiply(0)
+        multiply(1)
+        regroup_u(2)
+        regroup_u(3)
+        multiply(2)
+        multiply(3)
+        square_sum_of_xt(0)
+        dot_with_y(0)
+        square_sum_of_xt(1)
+        dot_with_y(1)
+        norm_of_xt(A)
+        square_sum_of_xt(2)
+        dot_with_y(2)
+        square_sum_of_xt(3)
+        dot_with_y(3)
+        norm_of_xt(B)
+        tanh_of_norm(ALL)
+        load_table(ACT.Ln, "warm_ln_b", col(r_norm, 3))
+        moebius_1(ALL)
+        moebius_2(ALL)
+        moebius_3(ALL)
+        moebius_4(ALL)
+        moebius_5(ALL)
+        moebius_6(ALL)
+        moebius_7(ALL)
+        root_of_r2(ALL)
+        direction(0)
+        relu_square_sum_on_scalar(0)
+        direction(1)
+        norm_and_unit_of_r2(ALL)
+        clip_of_r2(ALL)
+        relu_square_sum(1)
         log_of_r2(ALL)
-        load_table(ACT.Tanh, "warm_tanh_b")
-        relu_square_sums(PAIRS[1])
+        load_table(ACT.Tanh, "warm_tanh_b", col(ln_dn2, 3))
+        norm_of_relu(A)
+        direction(2)
+        direction(3)
+        artanh_of_r2(ALL)
+        relu_square_sum(2)
         log_map_coefficient(ALL)
-        out_coefficient(ALL)
-        finish(ALL)
+        norm_of_v(A)
+        tanh_of_v(A)
+        relu_square_sum(3)
+        reciprocal_of_relu(A)
+        norm_of_relu(B)
+        out_coefficient(A)
+        finish_on_scalar(0)
+        finish_on_scalar(1)
+        norm_of_v(B)
+        tanh_of_v(B)
+        reciprocal_of_relu(B)
+        out_coefficient(B)
+        finish(2)
+        finish(3)

@@ -21,9 +21,11 @@ TILES = N_ROWS // P
 BOUND = 1.0 - 168.0 * 2.0 ** -24
 ARTANH_BOUND = 0.5 * math.log((1.0 + BOUND) / (1.0 - BOUND))
 LN_EPS = 1e-5
+DEV_SCALE = 0.25 / (D * LN_EPS)
 NORM_MIN = 1e-15
 NORM_MIN_SQ = 1e-30
 SUM_SQ_MIN = 1e-20
+TANH_MAX = 1.0 - 2.0 ** -24
 
 FLOPS = 2 * N_ROWS * D * D
 
@@ -74,8 +76,8 @@ def tile_hnnlayer_s_kernel(tc, h, weight, bias, gamma, beta, out):
         beta_col = keep.tile([P, PACK], BF16, name="beta_col")
         bias_col = keep.tile([P, PACK], BF16, name="bias_col")
         nc.scalar.dma_start(out=gamma_col[:], in_=gamma.rearrange("(p t) -> p t", t=PACK))
-        nc.gpsimd.dma_start(out=beta_col[:], in_=beta.rearrange("(p t) -> p t", t=PACK))
-        nc.gpsimd.dma_start(out=bias_col[:], in_=bias.rearrange("o (p t) -> p (o t)", t=PACK))
+        nc.scalar.dma_start(out=beta_col[:], in_=beta.rearrange("(p t) -> p t", t=PACK))
+        nc.scalar.dma_start(out=bias_col[:], in_=bias.rearrange("o (p t) -> p (o t)", t=PACK))
         h_sb = keep.tile([P, TILES, D], BF16, name="h_sb")
         for i in range(TILES):
             nc.sync.dma_start(out=h_sb[:, i, :], in_=h[i * P : (i + 1) * P, :])
@@ -87,6 +89,8 @@ def tile_hnnlayer_s_kernel(tc, h, weight, bias, gamma, beta, out):
         nc.vector.memset(neg_half[:], -0.5)
         ones = one_number("ones")
         nc.vector.memset(ones[:], 1.0)
+        tiny = one_number("tiny")
+        nc.vector.memset(tiny[:], 2.0 ** -53)
         ident = keep.tile([P, P], BF16, name="ident")
         make_identity(nc, ident[:])
         ident_words = keep.tile([P, P], F32, name="ident_words")
@@ -134,48 +138,53 @@ def tile_hnnlayer_s_kernel(tc, h, weight, bias, gamma, beta, out):
         mean = row_numbers("mean")
         first_x2 = row_numbers("first_x2")
         first_sq = row_numbers("first_sq")
-        h_sq_a = row_numbers("h_sq_a")
         h_sq_b = row_numbers("h_sq_b")
         neg_sum_sq = row_numbers("neg_sum_sq")
         dev_sq = row_numbers("dev_sq")
         h_sq = row_numbers("h_sq")
         h_sq_clip = row_numbers("h_sq_clip")
         h_clip = row_numbers("h_clip")
-        eps_h_sq = row_numbers("eps_h_sq")
 
         def first_terms(rows):
             c = cols(rows)
             nc.vector.tensor_scalar_mul(out=first_x2[:, c], in0=first[:, c], scalar1=2.0)
-            nc.vector.scalar_tensor_tensor(
-                out=first_sq[:, c], in0=first[:, c], scalar=1.0 * D, in1=first[:, c],
-                op0=ALU.mult, op1=ALU.mult,
+            nc.scalar.activation(
+                out=first_sq[:, c], in_=first[:, c], func=ACT.Square, scale=math.sqrt(D),
+                bias=tiny[:],
             )
 
-        def norm_of_h(rows):
-            c = cols(rows)
-            nc.vector.tensor_mul(out=h_sq_a[:, c], in0=d_sum[:, c], in1=first_x2[:, c])
-            nc.vector.scalar_tensor_tensor(
-                out=mean[:, c], in0=d_sum[:, c], scalar=1.0 / D, in1=first[:, c],
+        def sums_of_h(i):
+            nc.vector.tensor_scalar(
+                out=col(h_sq_b, i), in0=col(d_sum, i), scalar1=col(first_x2, i),
+                scalar2=col(first_sq, i), op0=ALU.mult, op1=ALU.add,
+            )
+            nc.vector.tensor_scalar(
+                out=col(mean, i), in0=col(d_sum, i), scalar1=1.0 / D, scalar2=h_sb[:, i, 0:1],
                 op0=ALU.mult, op1=ALU.add,
             )
-            nc.vector.scalar_tensor_tensor(
-                out=neg_sum_sq[:, c], in0=d_sum[:, c], scalar=-1.0 / D, in1=d_sum[:, c],
-                op0=ALU.mult, op1=ALU.mult,
+            nc.vector.tensor_scalar(
+                out=col(neg_sum_sq, i), in0=col(d_sum, i), scalar1=-DEV_SCALE / D,
+                scalar2=col(d_sum, i), op0=ALU.mult, op1=ALU.mult,
             )
-            nc.vector.tensor_add(out=h_sq_b[:, c], in0=h_sq_a[:, c], in1=first_sq[:, c])
-            nc.vector.tensor_add(out=h_sq[:, c], in0=h_sq_b[:, c], in1=d_sq[:, c])
-            nc.vector.tensor_add(out=dev_sq[:, c], in0=neg_sum_sq[:, c], in1=d_sq[:, c])
-            nc.vector.tensor_scalar_min(out=h_sq_clip[:, c], in0=h_sq[:, c], scalar1=BOUND * BOUND)
+
+        def norm_of_h(i):
+            nc.vector.tensor_scalar(
+                out=col(h_sq_clip, i), in0=col(h_sq_b, i), scalar1=col(d_sq, i),
+                scalar2=BOUND * BOUND, op0=ALU.add, op1=ALU.min,
+            )
+
+        def deviation_of_h(i):
+            nc.scalar.activation(
+                out=col(h_sq, i), in_=col(d_sq, i), func=ACT.Identity, scale=1.0,
+                bias=col(h_sq_b, i),
+            )
+            nc.scalar.activation(
+                out=col(dev_sq, i), in_=col(d_sq, i), func=ACT.Identity, scale=DEV_SCALE,
+                bias=col(neg_sum_sq, i),
+            )
 
         def root_of_h(rows):
             power(h_clip, h_sq_clip, half, rows)
-
-        def eps_of_h(rows):
-            c = cols(rows)
-            nc.gpsimd.tensor_scalar(
-                out=eps_h_sq[:, c], in0=h_sq[:, c], scalar1=NORM_MIN_SQ, scalar2=4.0 * D * LN_EPS,
-                op0=ALU.max, op1=ALU.mult,
-            )
 
         centred = per_tile([P, D], F32, "centred")
 
@@ -204,19 +213,22 @@ def tile_hnnlayer_s_kernel(tc, h, weight, bias, gamma, beta, out):
                 )
             for i in rows:
                 nc.scalar.activation(
+                    out=col(theta2, i), in_=col(ln_dn, i), func=ACT.Identity,
+                    scale=-1.0, bias=col(ln_up, i),
+                )
+            for i in rows:
+                nc.scalar.activation(
                     out=col(k_arg, i), in_=col(theta_sq, i), func=ACT.Identity,
-                    scale=col(dev_sq, i), bias=col(eps_h_sq, i),
+                    scale=col(dev_sq, i), bias=col(h_sq, i),
                 )
 
         def root_of_k(rows):
             power(k_rsqrt, k_arg, neg_half, rows)
 
-        def layer_norm_factor(rows):
-            c = cols(rows)
-            nc.vector.tensor_sub(out=theta2[:, c], in0=ln_up[:, c], in1=ln_dn[:, c])
-            nc.vector.scalar_tensor_tensor(
-                out=k[:, c], in0=theta2[:, c], scalar=math.sqrt(D), in1=k_rsqrt[:, c],
-                op0=ALU.mult, op1=ALU.mult,
+        def layer_norm_factor(i):
+            nc.vector.tensor_scalar(
+                out=col(k, i), in0=col(theta2, i), scalar1=col(k_rsqrt, i),
+                scalar2=0.5 / math.sqrt(LN_EPS), op0=ALU.mult, op1=ALU.mult,
             )
 
         x = per_tile([P, D], F32, "x")
@@ -239,26 +251,28 @@ def tile_hnnlayer_s_kernel(tc, h, weight, bias, gamma, beta, out):
                 op0=ALU.mult, op1=ALU.mult, accum_out=col(x_sq, i),
             )
 
-        bias_sq = one_number("bias_sq")
         bias_sq_clip = one_number("bias_sq_clip")
         bias_norm = one_number("bias_norm")
         bias_rnorm = one_number("bias_rnorm")
         y_norm = one_number("y_norm")
-        y_scale = one_number("y_scale")
-        y_scale2 = one_number("y_scale2")
         neg_y_scale = one_number("neg_y_scale")
         y_sq = one_number("y_sq")
         one_plus_y_sq = one_number("one_plus_y_sq")
 
         def bias_square_sum():
-            products = scrap.tile([P, D], F32, name="products")
-            nc.vector.scalar_tensor_tensor(
-                out=products[:], in0=bias_bc[:], scalar=1.0, in1=bias_bc[:],
-                op0=ALU.mult, op1=ALU.mult, accum_out=bias_sq[:],
-            )
+            for t in range(PACK):
+                nc.tensor.matmul(
+                    out=xt[0][:, 0:1],
+                    lhsT=bias_col[:, t : t + 1].to_broadcast([P, P]),
+                    rhs=bias_col[:, t : t + 1],
+                    start=(t == 0),
+                    stop=(t == PACK - 1),
+                )
 
         def bias_norm_steps():
-            nc.gpsimd.tensor_scalar_max(out=bias_sq_clip[:], in0=bias_sq[:], scalar1=NORM_MIN_SQ)
+            nc.vector.tensor_scalar_max(
+                out=bias_sq_clip[:], in0=xt[0][:, 0:1], scalar1=NORM_MIN_SQ
+            )
             nc.gpsimd.tensor_tensor(
                 out=bias_norm[:], in0=bias_sq_clip[:], in1=half[:, 0:1], op=ALU.pow
             )
@@ -271,11 +285,6 @@ def tile_hnnlayer_s_kernel(tc, h, weight, bias, gamma, beta, out):
             nc.vector.tensor_mul(out=y_sq[:], in0=y_norm[:], in1=y_norm[:])
 
         def bias_point_2():
-            nc.vector.tensor_mul(out=y_scale[:], in0=y_norm[:], in1=bias_rnorm[:])
-            nc.vector.tensor_scalar(
-                out=y_scale2[:], in0=y_norm[:], scalar1=bias_rnorm[:], scalar2=2.0,
-                op0=ALU.mult, op1=ALU.mult,
-            )
             nc.vector.tensor_scalar(
                 out=neg_y_scale[:], in0=y_norm[:], scalar1=bias_rnorm[:], scalar2=-1.0,
                 op0=ALU.mult, op1=ALU.mult,
@@ -319,7 +328,7 @@ def tile_hnnlayer_s_kernel(tc, h, weight, bias, gamma, beta, out):
         u_scales = per_tile([P, P], U8, "u_scales")
         xt = [psum_keep.tile([P, D], F32, name="xt%d" % i) for i in range(TILES)]
         xt_sq = row_numbers("xt_sq")
-        xt_y2 = row_numbers("xt_y2")
+        neg_xt_y = row_numbers("neg_xt_y")
 
         def norm_of_x(rows):
             power(x_rnorm, x_sq, neg_half, rows)
@@ -334,16 +343,15 @@ def tile_hnnlayer_s_kernel(tc, h, weight, bias, gamma, beta, out):
         def make_u(i):
             nc.vector.tensor_scalar_mul(out=u[i][:], in0=x[i][:], scalar1=col(shrink, i))
             words = u[i][:].bitcast(F32)
-            if i % 2 == 0:
-                u_t[i // 2] = psum_tr.tile([P, 2, 2, P], F32, name="u_t", tag="tr")
+            u_t[i] = psum_tr.tile([P, 2, P], F32, name="u_t", tag="tr")
             for v in range(2):
                 nc.tensor.transpose(
-                    out=u_t[i // 2][:, i % 2, v, :], in_=words[:, v : D // 2 : 2], identity=ident_words[:]
+                    out=u_t[i][:, v, :], in_=words[:, v : D // 2 : 2], identity=ident_words[:]
                 )
 
         def regroup_u(i):
             nc.scalar.copy(
-                out=u_grouped[i][:].bitcast(F32), in_=u_t[i // 2][:, i % 2].rearrange("p v r -> p r v")
+                out=u_grouped[i][:].bitcast(F32), in_=u_t[i][:].rearrange("p v r -> p r v")
             )
 
         def multiply(i):
@@ -363,17 +371,20 @@ def tile_hnnlayer_s_kernel(tc, h, weight, bias, gamma, beta, out):
             )
 
         def square_sum_of_xt(i):
-            square_sum(xt[i][:], col(xt_sq, i))
+            squares = scrap.tile([P, D], BF16, name="squares")
+            nc.scalar.activation(
+                out=squares[:], in_=xt[i][:], func=ACT.Square, bias=tiny[:],
+                accum_out=col(xt_sq, i),
+            )
 
         def dot_with_y(i):
             products = scrap.tile([P, D], F32, name="products")
             nc.vector.scalar_tensor_tensor(
-                out=products[:], in0=xt[i][:], scalar=y_scale2[:], in1=bias_bc[:],
-                op0=ALU.mult, op1=ALU.mult, accum_out=col(xt_y2, i),
+                out=products[:], in0=xt[i][:], scalar=neg_y_scale[:], in1=bias_bc[:],
+                op0=ALU.mult, op1=ALU.mult, accum_out=col(neg_xt_y, i),
             )
 
         xt_norm = row_numbers("xt_norm")
-        xt_norm_clip = row_numbers("xt_norm_clip")
         r_norm = row_numbers("r_norm")
         xt_rnorm = row_numbers("xt_rnorm")
 
@@ -389,43 +400,44 @@ def tile_hnnlayer_s_kernel(tc, h, weight, bias, gamma, beta, out):
         r_sq = row_numbers("r_sq")
         y_coef = row_numbers("y_coef")
         xt_coef = row_numbers("xt_coef")
-        xt_rcoef = row_numbers("xt_rcoef")
-        bias_coef = row_numbers("bias_coef")
+        y_rcoef = row_numbers("y_rcoef")
+        xt_share = row_numbers("xt_share")
         den_m1 = row_numbers("den_m1")
         den = row_numbers("den")
         sum_sq = row_numbers("sum_sq")
         sum_den = row_numbers("sum_den")
         sum_den_rsqrt = row_numbers("sum_den_rsqrt")
-        r2_norm = row_numbers("r2_norm")
         r2_clip = row_numbers("r2_clip")
         z_unit = row_numbers("z_unit")
         ln_up2 = row_numbers("ln_up2")
         ln_dn2 = row_numbers("ln_dn2")
-        artanh2 = row_numbers("artanh2")
-        log_coef = row_numbers("log_coef")
+        log_coef2 = row_numbers("log_coef2")
 
         def moebius_1(rows):
             c = cols(rows)
-            nc.vector.tensor_scalar_max(out=xt_norm_clip[:, c], in0=xt_norm[:, c], scalar1=NORM_MIN)
+            nc.vector.reciprocal(out=xt_rnorm[:, c], in_=xt_norm[:, c])
+            nc.vector.scalar_tensor_tensor(
+                out=r_sq[:, c], in0=r_norm[:, c], scalar=TANH_MAX, in1=r_norm[:, c],
+                op0=ALU.min, op1=ALU.mult,
+            )
 
         def moebius_2(rows):
             c = cols(rows)
-            nc.vector.reciprocal(out=xt_rnorm[:, c], in_=xt_norm_clip[:, c])
+            nc.vector.tensor_mul(out=rho[:, c], in0=r_norm[:, c], in1=xt_rnorm[:, c])
+            nc.vector.tensor_scalar(
+                out=y_coef[:, c], in0=r_sq[:, c], scalar1=1.0, scalar2=neg_y_scale[:],
+                op0=ALU.subtract, op1=ALU.mult,
+            )
 
         def moebius_3(rows):
             c = cols(rows)
-            nc.vector.tensor_mul(out=rho[:, c], in0=r_norm[:, c], in1=xt_rnorm[:, c])
-            nc.vector.tensor_mul(out=r_sq[:, c], in0=r_norm[:, c], in1=r_norm[:, c])
+            nc.vector.scalar_tensor_tensor(
+                out=r_y2[:, c], in0=rho[:, c], scalar=-2.0, in1=neg_xt_y[:, c],
+                op0=ALU.mult, op1=ALU.mult,
+            )
+            nc.vector.reciprocal(out=y_rcoef[:, c], in_=y_coef[:, c])
 
         def moebius_4(rows):
-            c = cols(rows)
-            nc.vector.tensor_mul(out=r_y2[:, c], in0=rho[:, c], in1=xt_y2[:, c])
-            nc.vector.tensor_scalar(
-                out=y_coef[:, c], in0=r_sq[:, c], scalar1=neg_y_scale[:], scalar2=y_scale[:],
-                op0=ALU.mult, op1=ALU.add,
-            )
-
-        def moebius_5(rows):
             c = cols(rows)
             nc.vector.scalar_tensor_tensor(
                 out=xt_coef[:, c], in0=r_y2[:, c], scalar=one_plus_y_sq[:], in1=rho[:, c],
@@ -440,17 +452,16 @@ def tile_hnnlayer_s_kernel(tc, h, weight, bias, gamma, beta, out):
                 op0=ALU.add, op1=ALU.add,
             )
 
-        def moebius_6(rows):
+        def moebius_5(rows):
             c = cols(rows)
-            nc.vector.reciprocal(out=xt_rcoef[:, c], in_=xt_coef[:, c])
+            nc.vector.tensor_mul(out=xt_share[:, c], in0=xt_coef[:, c], in1=y_rcoef[:, c])
             nc.vector.tensor_scalar(
                 out=den[:, c], in0=den_m1[:, c], scalar1=1.0, scalar2=NORM_MIN,
                 op0=ALU.add, op1=ALU.max,
             )
 
-        def moebius_7(rows):
+        def moebius_6(rows):
             c = cols(rows)
-            nc.vector.tensor_mul(out=bias_coef[:, c], in0=y_coef[:, c], in1=xt_rcoef[:, c])
             nc.vector.scalar_tensor_tensor(
                 out=sum_den[:, c], in0=sum_sq[:, c], scalar=SUM_SQ_MIN, in1=den[:, c],
                 op0=ALU.max, op1=ALU.mult,
@@ -461,28 +472,25 @@ def tile_hnnlayer_s_kernel(tc, h, weight, bias, gamma, beta, out):
 
         def norm_and_unit_of_r2(rows):
             c = cols(rows)
-            nc.vector.tensor_mul(out=r2_norm[:, c], in0=sum_sq[:, c], in1=sum_den_rsqrt[:, c])
-            nc.vector.tensor_mul(out=z_unit[:, c], in0=xt_coef[:, c], in1=sum_den_rsqrt[:, c])
-
-        def clip_of_r2(rows):
-            c = cols(rows)
-            nc.vector.tensor_scalar_min(out=r2_clip[:, c], in0=r2_norm[:, c], scalar1=BOUND)
+            for i in rows:
+                nc.vector.tensor_scalar(
+                    out=col(r2_clip, i), in0=col(sum_sq, i), scalar1=col(sum_den_rsqrt, i),
+                    scalar2=BOUND, op0=ALU.mult, op1=ALU.min,
+                )
+            nc.vector.tensor_mul(out=z_unit[:, c], in0=y_coef[:, c], in1=sum_den_rsqrt[:, c])
 
         def log_of_r2(rows):
             c = cols(rows)
             nc.scalar.activation(out=ln_up2[:, c], in_=r2_clip[:, c], func=ACT.Ln, bias=1.0, scale=1.0)
             nc.scalar.activation(out=ln_dn2[:, c], in_=r2_clip[:, c], func=ACT.Ln, bias=1.0, scale=-1.0)
 
-        def artanh_of_r2(rows):
-            c = cols(rows)
-            nc.vector.tensor_sub(out=artanh2[:, c], in0=ln_up2[:, c], in1=ln_dn2[:, c])
-
         def log_map_coefficient(rows):
             c = cols(rows)
-            nc.vector.scalar_tensor_tensor(
-                out=log_coef[:, c], in0=artanh2[:, c], scalar=0.5, in1=z_unit[:, c],
-                op0=ALU.mult, op1=ALU.mult,
-            )
+            for i in rows:
+                nc.vector.tensor_scalar(
+                    out=col(log_coef2, i), in0=col(ln_up2, i), scalar1=col(ln_dn2, i),
+                    scalar2=col(z_unit, i), op0=ALU.subtract, op1=ALU.mult,
+                )
 
         z = per_tile([P, D], F32, "z")
         relu_sq = row_numbers("relu_sq")
@@ -490,7 +498,7 @@ def tile_hnnlayer_s_kernel(tc, h, weight, bias, gamma, beta, out):
 
         def direction(i):
             nc.vector.scalar_tensor_tensor(
-                out=z[i][:], in0=bias_bc[:], scalar=col(bias_coef, i), in1=xt[i][:],
+                out=z[i][:], in0=xt[i][:], scalar=col(xt_share, i), in1=bias_bc[:],
                 op0=ALU.mult, op1=ALU.add,
             )
 
@@ -506,10 +514,9 @@ def tile_hnnlayer_s_kernel(tc, h, weight, bias, gamma, beta, out):
             nc.scalar.activation(out=relu_z[:], in_=z[i][:], func=ACT.Relu)
             square_sum(relu_z[:], col(relu_sq, i))
 
-        v_norm = row_numbers("v_norm")
+        v_norm2 = row_numbers("v_norm2")
+        v_rnorm2 = row_numbers("v_rnorm2")
         v_tanh = row_numbers("v_tanh")
-        relu_norm_clip = row_numbers("relu_norm_clip")
-        relu_rnorm = row_numbers("relu_rnorm")
         out_coef = row_numbers("out_coef")
         result = per_tile([P, D], F32, "result")
 
@@ -519,24 +526,24 @@ def tile_hnnlayer_s_kernel(tc, h, weight, bias, gamma, beta, out):
         def norm_of_v(rows):
             c = cols(rows)
             nc.vector.scalar_tensor_tensor(
-                out=v_norm[:, c], in0=relu_norm[:, c], scalar=NORM_MIN, in1=log_coef[:, c],
+                out=v_norm2[:, c], in0=relu_norm[:, c], scalar=NORM_MIN, in1=log_coef2[:, c],
                 op0=ALU.max, op1=ALU.mult,
-            )
-            nc.vector.tensor_scalar_max(
-                out=relu_norm_clip[:, c], in0=relu_norm[:, c], scalar1=NORM_MIN
             )
 
         def tanh_of_v(rows):
             c = cols(rows)
-            nc.scalar.activation(out=v_tanh[:, c], in_=v_norm[:, c], func=ACT.Tanh)
+            nc.scalar.activation(out=v_tanh[:, c], in_=v_norm2[:, c], func=ACT.Tanh, scale=0.5)
 
-        def reciprocal_of_relu(rows):
+        def reciprocal_of_v(rows):
             c = cols(rows)
-            nc.vector.reciprocal(out=relu_rnorm[:, c], in_=relu_norm_clip[:, c])
+            nc.vector.reciprocal(out=v_rnorm2[:, c], in_=v_norm2[:, c])
 
         def out_coefficient(rows):
-            c = cols(rows)
-            nc.vector.tensor_mul(out=out_coef[:, c], in0=v_tanh[:, c], in1=relu_rnorm[:, c])
+            for i in rows:
+                nc.vector.tensor_scalar(
+                    out=col(out_coef, i), in0=col(v_tanh, i), scalar1=col(v_rnorm2, i),
+                    scalar2=col(log_coef2, i), op0=ALU.mult, op1=ALU.mult,
+                )
 
         def store(i):
             nc.sync.dma_start(out=out[i * P : (i + 1) * P, :], in_=result[i][:])
@@ -557,49 +564,63 @@ def tile_hnnlayer_s_kernel(tc, h, weight, bias, gamma, beta, out):
         B = range(2, 4)
 
         spread(gamma_col, affine_ps[:, 0])
+        bias_square_sum()
         shifted_square_sum(0)
         shifted_sum(0)
+        first_terms(A)
         shifted_square_sum(1)
         shifted_sum(1)
+        sums_of_h(0)
+        sums_of_h(1)
+        norm_of_h(0)
+        norm_of_h(1)
+        root_of_h(A)
+        bias_norm_steps()
         shifted_square_sum(2)
         shifted_sum(2)
-        first_terms(ALL)
+        first_terms(B)
+        deviation_of_h(0)
+        deviation_of_h(1)
         shifted_square_sum(3)
         shifted_sum(3)
-        spread(bias_col, bias_ps)
         spread(beta_col, affine_ps[:, 1])
-        collect_bias()
+        spread(bias_col, bias_ps)
         transpose_weight(0)
         transpose_weight(1)
-        norm_of_h(ALL)
-        root_of_h(ALL)
-        eps_of_h(ALL)
-        centre(0)
-        centre(1)
+        log_of_h(A)
+        root_of_k(A)
+        sums_of_h(2)
+        sums_of_h(3)
+        norm_of_h(2)
+        norm_of_h(3)
+        root_of_h(B)
+        deviation_of_h(2)
+        deviation_of_h(3)
         regroup_weight(0)
         regroup_weight(1)
-        log_of_h(ALL)
-        load_table(ACT.Tanh, "warm_tanh_a", col(k_arg, 3))
-        root_of_k(A)
+        collect_bias()
+        centre(0)
+        centre(1)
+        layer_norm_factor(0)
+        layer_norm_factor(1)
+        log_of_h(B)
         root_of_k(B)
-        centre(2)
-        centre(3)
-        bias_square_sum()
-        bias_norm_steps()
-        layer_norm_factor(A)
         layer_norm(0)
         layer_norm(1)
         square_sum_of_x(0)
         square_sum_of_x(1)
-        bias_tanh_step()
         norm_of_x(A)
-        layer_norm_factor(B)
+        load_table(ACT.Tanh, "warm_tanh_a", col(x_sq, 1))
+        bias_tanh_step()
+        centre(2)
+        centre(3)
+        layer_norm_factor(2)
+        layer_norm_factor(3)
         layer_norm(2)
         layer_norm(3)
         square_sum_of_x(2)
         square_sum_of_x(3)
         norm_of_x(B)
-        quantise_weight()
         shrink_factor(A)
         bias_point_1()
         make_u(0)
@@ -607,60 +628,69 @@ def tile_hnnlayer_s_kernel(tc, h, weight, bias, gamma, beta, out):
         bias_point_2()
         regroup_u(0)
         regroup_u(1)
+        quantise_weight()
+        multiply(0)
+        multiply(1)
         shrink_factor(B)
         make_u(2)
         make_u(3)
-        multiply(0)
-        multiply(1)
-        regroup_u(2)
-        regroup_u(3)
-        multiply(2)
-        multiply(3)
         square_sum_of_xt(0)
         dot_with_y(0)
+        regroup_u(2)
+        multiply(2)
         square_sum_of_xt(1)
         dot_with_y(1)
         norm_of_xt(A)
+        regroup_u(3)
+        multiply(3)
         square_sum_of_xt(2)
         dot_with_y(2)
+        tanh_of_norm(A)
         square_sum_of_xt(3)
-        dot_with_y(3)
         norm_of_xt(B)
-        tanh_of_norm(ALL)
-        load_table(ACT.Ln, "warm_ln_b", col(r_norm, 3))
-        moebius_1(ALL)
-        moebius_2(ALL)
-        moebius_3(ALL)
-        moebius_4(ALL)
-        moebius_5(ALL)
-        moebius_6(ALL)
-        moebius_7(ALL)
-        root_of_r2(ALL)
+        moebius_1(A)
+        moebius_2(A)
+        moebius_3(A)
+        dot_with_y(3)
+        moebius_4(A)
+        moebius_5(A)
+        moebius_6(A)
+        root_of_r2(A)
         direction(0)
-        relu_square_sum_on_scalar(0)
+        tanh_of_norm(B)
+        load_table(ACT.Ln, "warm_ln_b", col(r_norm, 3))
+        moebius_1(B)
         direction(1)
-        norm_and_unit_of_r2(ALL)
-        clip_of_r2(ALL)
-        relu_square_sum(1)
-        log_of_r2(ALL)
+        moebius_2(B)
+        relu_square_sum_on_scalar(0)
+        moebius_3(B)
+        norm_and_unit_of_r2(A)
+        moebius_4(B)
+        moebius_5(B)
+        moebius_6(B)
+        root_of_r2(B)
+        log_of_r2(A)
+        direction(2)
+        relu_square_sum_on_scalar(1)
+        direction(3)
+        norm_and_unit_of_r2(B)
+        log_of_r2(B)
         load_table(ACT.Tanh, "warm_tanh_b", col(ln_dn2, 3))
         norm_of_relu(A)
-        direction(2)
-        direction(3)
-        artanh_of_r2(ALL)
         relu_square_sum(2)
-        log_map_coefficient(ALL)
+        log_map_coefficient(A)
+        relu_square_sum(3)
         norm_of_v(A)
         tanh_of_v(A)
-        relu_square_sum(3)
-        reciprocal_of_relu(A)
         norm_of_relu(B)
+        log_map_coefficient(B)
+        reciprocal_of_v(A)
         out_coefficient(A)
         finish_on_scalar(0)
-        finish_on_scalar(1)
         norm_of_v(B)
         tanh_of_v(B)
-        reciprocal_of_relu(B)
+        finish_on_scalar(1)
+        reciprocal_of_v(B)
         out_coefficient(B)
         finish(2)
         finish(3)

@@ -25,7 +25,7 @@ DEV_SCALE = 0.25 / (D * LN_EPS)
 NORM_MIN = 1e-15
 NORM_MIN_SQ = 1e-30
 SUM_SQ_MIN = 1e-20
-TANH_MAX = 1.0 - 2.0 ** -24
+R_SQ_MAX = 1.0 - 2.0 ** -24
 
 FLOPS = 2 * N_ROWS * D * D
 
@@ -76,11 +76,11 @@ def tile_hnnlayer_s_kernel(tc, h, weight, bias, gamma, beta, out):
         beta_col = keep.tile([P, PACK], BF16, name="beta_col")
         bias_col = keep.tile([P, PACK], BF16, name="bias_col")
         nc.scalar.dma_start(out=gamma_col[:], in_=gamma.rearrange("(p t) -> p t", t=PACK))
-        nc.scalar.dma_start(out=beta_col[:], in_=beta.rearrange("(p t) -> p t", t=PACK))
-        nc.scalar.dma_start(out=bias_col[:], in_=bias.rearrange("o (p t) -> p (o t)", t=PACK))
         h_sb = keep.tile([P, TILES, D], BF16, name="h_sb")
         for i in range(TILES):
             nc.sync.dma_start(out=h_sb[:, i, :], in_=h[i * P : (i + 1) * P, :])
+        nc.sync.dma_start(out=bias_col[:], in_=bias.rearrange("o (p t) -> p (o t)", t=PACK))
+        nc.sync.dma_start(out=beta_col[:], in_=beta.rearrange("(p t) -> p t", t=PACK))
         w_sb = keep.tile([P, TILES, D], BF16, name="w_sb")
         nc.sync.dma_start(out=w_sb[:], in_=weight.rearrange("(o p) k -> p o k", p=P))
         half = row_numbers("half")
@@ -98,8 +98,7 @@ def tile_hnnlayer_s_kernel(tc, h, weight, bias, gamma, beta, out):
         load_table(ACT.Ln, "warm_ln", ones[:])
 
         affine_ps = psum_keep.tile([P, 2, PACK, P], BF16, name="affine_ps")
-        bias_ps = psum_tr.tile([P, PACK, P], BF16, name="bias_ps", tag="tr")
-        bias_bc = keep.tile([P, D], BF16, name="bias_bc")
+        bias_ps = []
         gamma_bc = affine_ps[:, 0].rearrange("q t p -> q p t")
         beta_bc = affine_ps[:, 1].rearrange("q t p -> q p t")
 
@@ -111,11 +110,10 @@ def tile_hnnlayer_s_kernel(tc, h, weight, bias, gamma, beta, out):
                     identity=ident[:],
                 )
 
-        def collect_bias():
-            nc.scalar.copy(
-                out=bias_bc[:].rearrange("q (p t) -> q p t", t=PACK),
-                in_=bias_ps[:].rearrange("q t p -> q p t"),
-            )
+        def spread_bias():
+            rows_ps = psum_tr.tile([P, PACK, P], BF16, name="bias_ps", tag="tr")
+            spread(bias_col, rows_ps)
+            bias_ps.append(rows_ps)
 
         first = h_sb[:, :, 0]
         d_sum = row_numbers("d_sum")
@@ -225,10 +223,11 @@ def tile_hnnlayer_s_kernel(tc, h, weight, bias, gamma, beta, out):
         def root_of_k(rows):
             power(k_rsqrt, k_arg, neg_half, rows)
 
-        def layer_norm_factor(i):
-            nc.vector.tensor_scalar(
-                out=col(k, i), in0=col(theta2, i), scalar1=col(k_rsqrt, i),
-                scalar2=0.5 / math.sqrt(LN_EPS), op0=ALU.mult, op1=ALU.mult,
+        def layer_norm_factor(rows):
+            c = cols(rows)
+            nc.vector.scalar_tensor_tensor(
+                out=k[:, c], in0=theta2[:, c], scalar=0.5 / math.sqrt(LN_EPS),
+                in1=k_rsqrt[:, c], op0=ALU.mult, op1=ALU.mult,
             )
 
         x = per_tile([P, D], F32, "x")
@@ -255,9 +254,11 @@ def tile_hnnlayer_s_kernel(tc, h, weight, bias, gamma, beta, out):
         bias_norm = one_number("bias_norm")
         bias_rnorm = one_number("bias_rnorm")
         y_norm = one_number("y_norm")
-        neg_y_scale = one_number("neg_y_scale")
+        y_scale = one_number("y_scale")
         y_sq = one_number("y_sq")
-        one_plus_y_sq = one_number("one_plus_y_sq")
+        y_sq_p1 = one_number("y_sq_p1")
+        y_sq_m1 = one_number("y_sq_m1")
+        y_bc = keep.tile([P, D], F32, name="y_bc")
 
         def bias_square_sum():
             for t in range(PACK):
@@ -277,19 +278,23 @@ def tile_hnnlayer_s_kernel(tc, h, weight, bias, gamma, beta, out):
                 out=bias_norm[:], in0=bias_sq_clip[:], in1=half[:, 0:1], op=ALU.pow
             )
 
-        def bias_tanh_step():
-            nc.scalar.activation(out=y_norm[:], in_=bias_norm[:], func=ACT.Tanh)
-
-        def bias_point_1():
+        def bias_reciprocal():
             nc.vector.reciprocal(out=bias_rnorm[:], in_=bias_norm[:])
-            nc.vector.tensor_mul(out=y_sq[:], in0=y_norm[:], in1=y_norm[:])
 
-        def bias_point_2():
-            nc.vector.tensor_scalar(
-                out=neg_y_scale[:], in0=y_norm[:], scalar1=bias_rnorm[:], scalar2=-1.0,
-                op0=ALU.mult, op1=ALU.mult,
+        def bias_point():
+            nc.scalar.activation(out=y_norm[:], in_=bias_norm[:], func=ACT.Tanh)
+            nc.scalar.activation(
+                out=y_scale[:], in_=y_norm[:], func=ACT.Identity, scale=bias_rnorm[:]
             )
-            nc.vector.tensor_scalar_add(out=one_plus_y_sq[:], in0=y_sq[:], scalar1=1.0)
+            nc.gpsimd.tensor_tensor(out=y_sq[:], in0=y_norm[:], in1=y_norm[:], op=ALU.mult)
+            nc.gpsimd.tensor_scalar_add(out=y_sq_p1[:], in0=y_sq[:], scalar1=1.0)
+            nc.gpsimd.tensor_scalar_add(out=y_sq_m1[:], in0=y_sq[:], scalar1=-1.0)
+
+        def collect_y():
+            nc.scalar.activation(
+                out=by_four(y_bc[:]), in_=bias_ps[0][:].rearrange("q t p -> q p t"),
+                func=ACT.Identity, scale=y_scale[:],
+            )
 
         w_grouped = keep.tile([P, D, PACK], BF16, name="w_grouped", align_bytes=64)
         w_codes = keep.tile([P, D], U32, name="w_codes", align_bytes=64)
@@ -328,7 +333,7 @@ def tile_hnnlayer_s_kernel(tc, h, weight, bias, gamma, beta, out):
         u_scales = per_tile([P, P], U8, "u_scales")
         xt = [psum_keep.tile([P, D], F32, name="xt%d" % i) for i in range(TILES)]
         xt_sq = row_numbers("xt_sq")
-        neg_xt_y = row_numbers("neg_xt_y")
+        xt_y2 = row_numbers("xt_y2")
 
         def norm_of_x(rows):
             power(x_rnorm, x_sq, neg_half, rows)
@@ -380,8 +385,8 @@ def tile_hnnlayer_s_kernel(tc, h, weight, bias, gamma, beta, out):
         def dot_with_y(i):
             products = scrap.tile([P, D], F32, name="products")
             nc.vector.scalar_tensor_tensor(
-                out=products[:], in0=xt[i][:], scalar=neg_y_scale[:], in1=bias_bc[:],
-                op0=ALU.mult, op1=ALU.mult, accum_out=col(neg_xt_y, i),
+                out=products[:], in0=xt[i][:], scalar=2.0, in1=y_bc[:],
+                op0=ALU.mult, op1=ALU.mult, accum_out=col(xt_y2, i),
             )
 
         xt_norm = row_numbers("xt_norm")
@@ -394,15 +399,15 @@ def tile_hnnlayer_s_kernel(tc, h, weight, bias, gamma, beta, out):
         def tanh_of_norm(rows):
             c = cols(rows)
             nc.scalar.activation(out=r_norm[:, c], in_=xt_norm[:, c], func=ACT.Tanh)
+            nc.scalar.activation(out=r_sq[:, c], in_=r_norm[:, c], func=ACT.Square)
 
         r_y2 = row_numbers("r_y2")
         rho = row_numbers("rho")
         r_sq = row_numbers("r_sq")
-        y_coef = row_numbers("y_coef")
+        r_sq_m1 = row_numbers("r_sq_m1")
+        r_sq_rm1 = row_numbers("r_sq_rm1")
         xt_coef = row_numbers("xt_coef")
-        y_rcoef = row_numbers("y_rcoef")
         xt_share = row_numbers("xt_share")
-        den_m1 = row_numbers("den_m1")
         den = row_numbers("den")
         sum_sq = row_numbers("sum_sq")
         sum_den = row_numbers("sum_den")
@@ -416,36 +421,25 @@ def tile_hnnlayer_s_kernel(tc, h, weight, bias, gamma, beta, out):
         def moebius_1(rows):
             c = cols(rows)
             nc.vector.reciprocal(out=xt_rnorm[:, c], in_=xt_norm[:, c])
-            nc.vector.scalar_tensor_tensor(
-                out=r_sq[:, c], in0=r_norm[:, c], scalar=TANH_MAX, in1=r_norm[:, c],
-                op0=ALU.min, op1=ALU.mult,
-            )
 
         def moebius_2(rows):
             c = cols(rows)
             nc.vector.tensor_mul(out=rho[:, c], in0=r_norm[:, c], in1=xt_rnorm[:, c])
             nc.vector.tensor_scalar(
-                out=y_coef[:, c], in0=r_sq[:, c], scalar1=1.0, scalar2=neg_y_scale[:],
-                op0=ALU.subtract, op1=ALU.mult,
+                out=r_sq_m1[:, c], in0=r_sq[:, c], scalar1=R_SQ_MAX, scalar2=-1.0,
+                op0=ALU.min, op1=ALU.add,
             )
 
         def moebius_3(rows):
             c = cols(rows)
-            nc.vector.scalar_tensor_tensor(
-                out=r_y2[:, c], in0=rho[:, c], scalar=-2.0, in1=neg_xt_y[:, c],
-                op0=ALU.mult, op1=ALU.mult,
-            )
-            nc.vector.reciprocal(out=y_rcoef[:, c], in_=y_coef[:, c])
+            nc.vector.tensor_mul(out=r_y2[:, c], in0=rho[:, c], in1=xt_y2[:, c])
+            nc.vector.reciprocal(out=r_sq_rm1[:, c], in_=r_sq_m1[:, c])
 
         def moebius_4(rows):
             c = cols(rows)
             nc.vector.scalar_tensor_tensor(
-                out=xt_coef[:, c], in0=r_y2[:, c], scalar=one_plus_y_sq[:], in1=rho[:, c],
+                out=xt_coef[:, c], in0=r_y2[:, c], scalar=y_sq_p1[:], in1=rho[:, c],
                 op0=ALU.add, op1=ALU.mult,
-            )
-            nc.vector.scalar_tensor_tensor(
-                out=den_m1[:, c], in0=r_sq[:, c], scalar=y_sq[:], in1=r_y2[:, c],
-                op0=ALU.mult, op1=ALU.add,
             )
             nc.vector.scalar_tensor_tensor(
                 out=sum_sq[:, c], in0=r_sq[:, c], scalar=y_sq[:], in1=r_y2[:, c],
@@ -454,10 +448,13 @@ def tile_hnnlayer_s_kernel(tc, h, weight, bias, gamma, beta, out):
 
         def moebius_5(rows):
             c = cols(rows)
-            nc.vector.tensor_mul(out=xt_share[:, c], in0=xt_coef[:, c], in1=y_rcoef[:, c])
-            nc.vector.tensor_scalar(
-                out=den[:, c], in0=den_m1[:, c], scalar1=1.0, scalar2=NORM_MIN,
-                op0=ALU.add, op1=ALU.max,
+            nc.vector.scalar_tensor_tensor(
+                out=xt_share[:, c], in0=xt_coef[:, c], scalar=-1.0, in1=r_sq_rm1[:, c],
+                op0=ALU.mult, op1=ALU.mult,
+            )
+            nc.vector.scalar_tensor_tensor(
+                out=den[:, c], in0=r_sq_m1[:, c], scalar=y_sq_m1[:], in1=sum_sq[:, c],
+                op0=ALU.mult, op1=ALU.add,
             )
 
         def moebius_6(rows):
@@ -477,7 +474,10 @@ def tile_hnnlayer_s_kernel(tc, h, weight, bias, gamma, beta, out):
                     out=col(r2_clip, i), in0=col(sum_sq, i), scalar1=col(sum_den_rsqrt, i),
                     scalar2=BOUND, op0=ALU.mult, op1=ALU.min,
                 )
-            nc.vector.tensor_mul(out=z_unit[:, c], in0=y_coef[:, c], in1=sum_den_rsqrt[:, c])
+            nc.vector.scalar_tensor_tensor(
+                out=z_unit[:, c], in0=r_sq_m1[:, c], scalar=-1.0, in1=sum_den_rsqrt[:, c],
+                op0=ALU.mult, op1=ALU.mult,
+            )
 
         def log_of_r2(rows):
             c = cols(rows)
@@ -485,7 +485,6 @@ def tile_hnnlayer_s_kernel(tc, h, weight, bias, gamma, beta, out):
             nc.scalar.activation(out=ln_dn2[:, c], in_=r2_clip[:, c], func=ACT.Ln, bias=1.0, scale=-1.0)
 
         def log_map_coefficient(rows):
-            c = cols(rows)
             for i in rows:
                 nc.vector.tensor_scalar(
                     out=col(log_coef2, i), in0=col(ln_up2, i), scalar1=col(ln_dn2, i),
@@ -498,7 +497,7 @@ def tile_hnnlayer_s_kernel(tc, h, weight, bias, gamma, beta, out):
 
         def direction(i):
             nc.vector.scalar_tensor_tensor(
-                out=z[i][:], in0=xt[i][:], scalar=col(xt_share, i), in1=bias_bc[:],
+                out=z[i][:], in0=xt[i][:], scalar=col(xt_share, i), in1=y_bc[:],
                 op0=ALU.mult, op1=ALU.add,
             )
 
@@ -509,10 +508,14 @@ def tile_hnnlayer_s_kernel(tc, h, weight, bias, gamma, beta, out):
                 op0=ALU.max, op1=ALU.mult, accum_out=col(relu_sq, i),
             )
 
+        relu_z = {}
+
+        def relu_on_scalar(i):
+            relu_z[i] = scrap.tile([P, D], F32, name="relu_z")
+            nc.scalar.activation(out=relu_z[i][:], in_=z[i][:], func=ACT.Relu)
+
         def relu_square_sum_on_scalar(i):
-            relu_z = scrap.tile([P, D], F32, name="relu_z")
-            nc.scalar.activation(out=relu_z[:], in_=z[i][:], func=ACT.Relu)
-            square_sum(relu_z[:], col(relu_sq, i))
+            square_sum(relu_z[i][:], col(relu_sq, i))
 
         v_norm2 = row_numbers("v_norm2")
         v_rnorm2 = row_numbers("v_rnorm2")
@@ -564,7 +567,6 @@ def tile_hnnlayer_s_kernel(tc, h, weight, bias, gamma, beta, out):
         B = range(2, 4)
 
         spread(gamma_col, affine_ps[:, 0])
-        bias_square_sum()
         shifted_square_sum(0)
         shifted_sum(0)
         first_terms(A)
@@ -575,7 +577,6 @@ def tile_hnnlayer_s_kernel(tc, h, weight, bias, gamma, beta, out):
         norm_of_h(0)
         norm_of_h(1)
         root_of_h(A)
-        bias_norm_steps()
         shifted_square_sum(2)
         shifted_sum(2)
         first_terms(B)
@@ -584,9 +585,10 @@ def tile_hnnlayer_s_kernel(tc, h, weight, bias, gamma, beta, out):
         shifted_square_sum(3)
         shifted_sum(3)
         spread(beta_col, affine_ps[:, 1])
-        spread(bias_col, bias_ps)
+        bias_square_sum()
         transpose_weight(0)
         transpose_weight(1)
+        spread_bias()
         log_of_h(A)
         root_of_k(A)
         sums_of_h(2)
@@ -594,40 +596,38 @@ def tile_hnnlayer_s_kernel(tc, h, weight, bias, gamma, beta, out):
         norm_of_h(2)
         norm_of_h(3)
         root_of_h(B)
+        bias_norm_steps()
         deviation_of_h(2)
         deviation_of_h(3)
         regroup_weight(0)
         regroup_weight(1)
-        collect_bias()
         centre(0)
         centre(1)
-        layer_norm_factor(0)
-        layer_norm_factor(1)
+        layer_norm_factor(A)
         log_of_h(B)
         root_of_k(B)
         layer_norm(0)
         layer_norm(1)
+        bias_reciprocal()
         square_sum_of_x(0)
         square_sum_of_x(1)
         norm_of_x(A)
         load_table(ACT.Tanh, "warm_tanh_a", col(x_sq, 1))
-        bias_tanh_step()
         centre(2)
         centre(3)
-        layer_norm_factor(2)
-        layer_norm_factor(3)
+        layer_norm_factor(B)
         layer_norm(2)
+        shrink_factor(A)
         layer_norm(3)
         square_sum_of_x(2)
         square_sum_of_x(3)
         norm_of_x(B)
-        shrink_factor(A)
-        bias_point_1()
+        bias_point()
         make_u(0)
         make_u(1)
-        bias_point_2()
         regroup_u(0)
         regroup_u(1)
+        collect_y()
         quantise_weight()
         multiply(0)
         multiply(1)
@@ -662,7 +662,8 @@ def tile_hnnlayer_s_kernel(tc, h, weight, bias, gamma, beta, out):
         moebius_1(B)
         direction(1)
         moebius_2(B)
-        relu_square_sum_on_scalar(0)
+        relu_on_scalar(0)
+        relu_on_scalar(1)
         moebius_3(B)
         norm_and_unit_of_r2(A)
         moebius_4(B)
@@ -671,6 +672,7 @@ def tile_hnnlayer_s_kernel(tc, h, weight, bias, gamma, beta, out):
         root_of_r2(B)
         log_of_r2(A)
         direction(2)
+        relu_square_sum_on_scalar(0)
         relu_square_sum_on_scalar(1)
         direction(3)
         norm_and_unit_of_r2(B)
@@ -686,11 +688,11 @@ def tile_hnnlayer_s_kernel(tc, h, weight, bias, gamma, beta, out):
         log_map_coefficient(B)
         reciprocal_of_v(A)
         out_coefficient(A)
-        finish_on_scalar(0)
         norm_of_v(B)
+        finish(0)
         tanh_of_v(B)
-        finish_on_scalar(1)
         reciprocal_of_v(B)
+        finish_on_scalar(1)
         out_coefficient(B)
         finish(2)
         finish(3)

@@ -224,11 +224,11 @@ def tile_hnnlayer_s_kernel(tc, h, weight, bias, gamma, beta, out):
             power(k_rsqrt, k_arg, neg_half, rows)
 
         def layer_norm_factor(rows):
-            c = cols(rows)
-            nc.vector.scalar_tensor_tensor(
-                out=k[:, c], in0=theta2[:, c], scalar=0.5 / math.sqrt(LN_EPS),
-                in1=k_rsqrt[:, c], op0=ALU.mult, op1=ALU.mult,
-            )
+            for i in rows:
+                nc.vector.tensor_scalar(
+                    out=col(k, i), in0=col(theta2, i), scalar1=col(k_rsqrt, i),
+                    scalar2=0.5 / math.sqrt(LN_EPS), op0=ALU.mult, op1=ALU.mult,
+                )
 
         x = per_tile([P, D], F32, "x")
         x_sq = row_numbers("x_sq")
@@ -286,9 +286,14 @@ def tile_hnnlayer_s_kernel(tc, h, weight, bias, gamma, beta, out):
             nc.scalar.activation(
                 out=y_scale[:], in_=y_norm[:], func=ACT.Identity, scale=bias_rnorm[:]
             )
-            nc.gpsimd.tensor_tensor(out=y_sq[:], in0=y_norm[:], in1=y_norm[:], op=ALU.mult)
-            nc.gpsimd.tensor_scalar_add(out=y_sq_p1[:], in0=y_sq[:], scalar1=1.0)
-            nc.gpsimd.tensor_scalar_add(out=y_sq_m1[:], in0=y_sq[:], scalar1=-1.0)
+
+        def bias_squares():
+            nc.vector.tensor_scalar_mul(out=y_sq[:], in0=y_norm[:], scalar1=y_norm[:])
+            for total, offset in ((y_sq_p1, 1.0), (y_sq_m1, -1.0)):
+                nc.vector.tensor_scalar(
+                    out=total[:], in0=y_norm[:], scalar1=y_norm[:], scalar2=offset,
+                    op0=ALU.mult, op1=ALU.add,
+                )
 
         def collect_y():
             nc.scalar.activation(
@@ -527,11 +532,11 @@ def tile_hnnlayer_s_kernel(tc, h, weight, bias, gamma, beta, out):
             power(relu_norm, relu_sq, half, rows)
 
         def norm_of_v(rows):
-            c = cols(rows)
-            nc.vector.scalar_tensor_tensor(
-                out=v_norm2[:, c], in0=relu_norm[:, c], scalar=NORM_MIN, in1=log_coef2[:, c],
-                op0=ALU.max, op1=ALU.mult,
-            )
+            for i in rows:
+                nc.vector.tensor_scalar(
+                    out=col(v_norm2, i), in0=col(relu_norm, i), scalar1=NORM_MIN,
+                    scalar2=col(log_coef2, i), op0=ALU.max, op1=ALU.mult,
+                )
 
         def tanh_of_v(rows):
             c = cols(rows)
@@ -634,26 +639,27 @@ def tile_hnnlayer_s_kernel(tc, h, weight, bias, gamma, beta, out):
         shrink_factor(B)
         make_u(2)
         make_u(3)
+        bias_squares()
         square_sum_of_xt(0)
+        square_sum_of_xt(1)
+        norm_of_xt(A)
         dot_with_y(0)
         regroup_u(2)
-        multiply(2)
-        square_sum_of_xt(1)
-        dot_with_y(1)
-        norm_of_xt(A)
         regroup_u(3)
+        multiply(2)
         multiply(3)
-        square_sum_of_xt(2)
-        dot_with_y(2)
+        dot_with_y(1)
         tanh_of_norm(A)
+        moebius_1(A)
+        square_sum_of_xt(2)
+        moebius_2(A)
         square_sum_of_xt(3)
         norm_of_xt(B)
-        moebius_1(A)
-        moebius_2(A)
         moebius_3(A)
-        dot_with_y(3)
+        dot_with_y(2)
         moebius_4(A)
         moebius_5(A)
+        dot_with_y(3)
         moebius_6(A)
         root_of_r2(A)
         direction(0)
@@ -688,8 +694,8 @@ def tile_hnnlayer_s_kernel(tc, h, weight, bias, gamma, beta, out):
         log_map_coefficient(B)
         reciprocal_of_v(A)
         out_coefficient(A)
-        norm_of_v(B)
         finish(0)
+        norm_of_v(B)
         tanh_of_v(B)
         reciprocal_of_v(B)
         finish_on_scalar(1)

@@ -22,6 +22,8 @@ BOUND = 1.0 - 168.0 * 2.0 ** -24
 ARTANH_BOUND = 0.5 * math.log((1.0 + BOUND) / (1.0 - BOUND))
 LN_EPS = 1e-5
 DEV_SCALE = 0.25 / (D * LN_EPS)
+K_SCALE = 0.5 / math.sqrt(LN_EPS)
+TWO_LOG2E = 2.0 / math.log(2.0)
 NORM_MIN = 1e-15
 NORM_MIN_SQ = 1e-30
 SUM_SQ_MIN = 1e-20
@@ -89,6 +91,10 @@ def tile_hnnlayer_s_kernel(tc, h, weight, bias, gamma, beta, out):
         nc.vector.memset(neg_half[:], -0.5)
         ones = one_number("ones")
         nc.vector.memset(ones[:], 1.0)
+        neg_one = one_number("neg_one")
+        nc.vector.memset(neg_one[:], -1.0)
+        two = one_number("two")
+        nc.vector.memset(two[:], 2.0)
         tiny = one_number("tiny")
         nc.vector.memset(tiny[:], 2.0 ** -53)
         ident = keep.tile([P, P], BF16, name="ident")
@@ -136,11 +142,11 @@ def tile_hnnlayer_s_kernel(tc, h, weight, bias, gamma, beta, out):
         mean = row_numbers("mean")
         first_x2 = row_numbers("first_x2")
         first_sq = row_numbers("first_sq")
-        h_sq_b = row_numbers("h_sq_b")
+        h_sq_b = [keep.tile([P, 2], F32, name="h_sq_b%d" % pair) for pair in range(2)]
+        h_sq_clip = [keep.tile([P, 2], F32, name="h_sq_clip%d" % pair) for pair in range(2)]
         neg_sum_sq = row_numbers("neg_sum_sq")
         dev_sq = row_numbers("dev_sq")
         h_sq = row_numbers("h_sq")
-        h_sq_clip = row_numbers("h_sq_clip")
         h_clip = row_numbers("h_clip")
 
         def first_terms(rows):
@@ -151,11 +157,7 @@ def tile_hnnlayer_s_kernel(tc, h, weight, bias, gamma, beta, out):
                 bias=tiny[:],
             )
 
-        def sums_of_h(i):
-            nc.vector.tensor_scalar(
-                out=col(h_sq_b, i), in0=col(d_sum, i), scalar1=col(first_x2, i),
-                scalar2=col(first_sq, i), op0=ALU.mult, op1=ALU.add,
-            )
+        def mean_of_h(i):
             nc.vector.tensor_scalar(
                 out=col(mean, i), in0=col(d_sum, i), scalar1=1.0 / D, scalar2=h_sb[:, i, 0:1],
                 op0=ALU.mult, op1=ALU.add,
@@ -165,16 +167,22 @@ def tile_hnnlayer_s_kernel(tc, h, weight, bias, gamma, beta, out):
                 scalar2=col(d_sum, i), op0=ALU.mult, op1=ALU.mult,
             )
 
-        def norm_of_h(i):
-            nc.vector.tensor_scalar(
-                out=col(h_sq_clip, i), in0=col(h_sq_b, i), scalar1=col(d_sq, i),
-                scalar2=BOUND * BOUND, op0=ALU.add, op1=ALU.min,
+        def terms_of_h(i, engine):
+            engine.tensor_scalar(
+                out=col(h_sq_b[i // 2], i % 2), in0=col(d_sum, i), scalar1=col(first_x2, i),
+                scalar2=col(first_sq, i), op0=ALU.mult, op1=ALU.add,
+            )
+
+        def clip_of_h(i, engine):
+            engine.tensor_scalar(
+                out=col(h_sq_clip[i // 2], i % 2), in0=col(h_sq_b[i // 2], i % 2),
+                scalar1=col(d_sq, i), scalar2=BOUND * BOUND, op0=ALU.add, op1=ALU.min,
             )
 
         def deviation_of_h(i):
             nc.scalar.activation(
                 out=col(h_sq, i), in_=col(d_sq, i), func=ACT.Identity, scale=1.0,
-                bias=col(h_sq_b, i),
+                bias=col(h_sq_b[i // 2], i % 2),
             )
             nc.scalar.activation(
                 out=col(dev_sq, i), in_=col(d_sq, i), func=ACT.Identity, scale=DEV_SCALE,
@@ -182,7 +190,10 @@ def tile_hnnlayer_s_kernel(tc, h, weight, bias, gamma, beta, out):
             )
 
         def root_of_h(rows):
-            power(h_clip, h_sq_clip, half, rows)
+            c = cols(rows)
+            nc.gpsimd.tensor_tensor(
+                out=h_clip[:, c], in0=h_sq_clip[rows[0] // 2][:], in1=half[:, c], op=ALU.pow
+            )
 
         centred = per_tile([P, D], F32, "centred")
 
@@ -195,6 +206,7 @@ def tile_hnnlayer_s_kernel(tc, h, weight, bias, gamma, beta, out):
         ln_up = row_numbers("ln_up")
         ln_dn = row_numbers("ln_dn")
         theta_sq = row_numbers("theta_sq")
+        ln_up_scaled = row_numbers("ln_up_scaled")
         theta2 = row_numbers("theta2")
         k_arg = row_numbers("k_arg")
         k_rsqrt = row_numbers("k_rsqrt")
@@ -209,15 +221,18 @@ def tile_hnnlayer_s_kernel(tc, h, weight, bias, gamma, beta, out):
                     out=col(theta_sq, i), in_=col(ln_dn, i), func=ACT.Square,
                     scale=-1.0, bias=col(ln_up, i),
                 )
-            for i in rows:
-                nc.scalar.activation(
-                    out=col(theta2, i), in_=col(ln_dn, i), func=ACT.Identity,
-                    scale=-1.0, bias=col(ln_up, i),
-                )
+            nc.scalar.activation(
+                out=ln_up_scaled[:, c], in_=ln_up[:, c], func=ACT.Identity, scale=K_SCALE
+            )
             for i in rows:
                 nc.scalar.activation(
                     out=col(k_arg, i), in_=col(theta_sq, i), func=ACT.Identity,
                     scale=col(dev_sq, i), bias=col(h_sq, i),
+                )
+            for i in rows:
+                nc.scalar.activation(
+                    out=col(theta2, i), in_=col(ln_dn, i), func=ACT.Identity,
+                    scale=-K_SCALE, bias=col(ln_up_scaled, i),
                 )
 
         def root_of_k(rows):
@@ -225,9 +240,8 @@ def tile_hnnlayer_s_kernel(tc, h, weight, bias, gamma, beta, out):
 
         def layer_norm_factor(rows):
             for i in rows:
-                nc.vector.tensor_scalar(
-                    out=col(k, i), in0=col(theta2, i), scalar1=col(k_rsqrt, i),
-                    scalar2=0.5 / math.sqrt(LN_EPS), op0=ALU.mult, op1=ALU.mult,
+                nc.scalar.activation(
+                    out=col(k, i), in_=col(k_rsqrt, i), func=ACT.Identity, scale=col(theta2, i)
                 )
 
         x = per_tile([P, D], F32, "x")
@@ -251,8 +265,11 @@ def tile_hnnlayer_s_kernel(tc, h, weight, bias, gamma, beta, out):
             )
 
         bias_sq_clip = one_number("bias_sq_clip")
-        bias_norm = one_number("bias_norm")
-        bias_rnorm = one_number("bias_rnorm")
+        bias_log2 = one_number("bias_log2")
+        bias_rlog2 = one_number("bias_rlog2")
+        bias_exp = one_number("bias_exp")
+        bias_exp_p1 = one_number("bias_exp_p1")
+        bias_rexp = one_number("bias_rexp")
         y_norm = one_number("y_norm")
         y_scale = one_number("y_scale")
         y_sq = one_number("y_sq")
@@ -270,21 +287,42 @@ def tile_hnnlayer_s_kernel(tc, h, weight, bias, gamma, beta, out):
                     stop=(t == PACK - 1),
                 )
 
-        def bias_norm_steps():
-            nc.vector.tensor_scalar_max(
-                out=bias_sq_clip[:], in0=xt[0][:, 0:1], scalar1=NORM_MIN_SQ
+        def bias_clip():
+            nc.vector.tensor_scalar(
+                out=bias_sq_clip[:], in0=xt[0][:, 0:1], scalar1=NORM_MIN_SQ,
+                scalar2=TWO_LOG2E * TWO_LOG2E, op0=ALU.max, op1=ALU.mult,
             )
-            nc.gpsimd.tensor_tensor(
-                out=bias_norm[:], in0=bias_sq_clip[:], in1=half[:, 0:1], op=ALU.pow
+
+        def gpsimd_power(dst, base, exponent):
+            nc.gpsimd.tensor_tensor(out=dst[:], in0=base, in1=exponent, op=ALU.pow)
+
+        def bias_root():
+            gpsimd_power(bias_log2, bias_sq_clip[:], half[:, 0:1])
+
+        def bias_exponential():
+            gpsimd_power(bias_exp, two[:], bias_log2[:])
+
+        def bias_tanh():
+            nc.gpsimd.tensor_scalar_add(out=bias_exp_p1[:], in0=bias_exp[:], scalar1=1.0)
+            gpsimd_power(bias_rexp, bias_exp_p1[:], neg_one[:])
+            nc.gpsimd.tensor_scalar(
+                out=y_norm[:], in0=bias_rexp[:], scalar1=-2.0, scalar2=1.0,
+                op0=ALU.mult, op1=ALU.add,
             )
 
         def bias_reciprocal():
-            nc.vector.reciprocal(out=bias_rnorm[:], in_=bias_norm[:])
+            nc.vector.reciprocal(out=bias_rlog2[:], in_=bias_log2[:])
 
-        def bias_point():
-            nc.scalar.activation(out=y_norm[:], in_=bias_norm[:], func=ACT.Tanh)
+        def scale_of_y():
+            nc.vector.tensor_scalar(
+                out=y_scale[:], in0=y_norm[:], scalar1=bias_rlog2[:], scalar2=TWO_LOG2E,
+                op0=ALU.mult, op1=ALU.mult,
+            )
+
+        def collect_y():
             nc.scalar.activation(
-                out=y_scale[:], in_=y_norm[:], func=ACT.Identity, scale=bias_rnorm[:]
+                out=by_four(y_bc[:]), in_=bias_ps[0][:].rearrange("q t p -> q p t"),
+                func=ACT.Identity, scale=y_scale[:],
             )
 
         def bias_squares():
@@ -294,12 +332,6 @@ def tile_hnnlayer_s_kernel(tc, h, weight, bias, gamma, beta, out):
                     out=total[:], in0=y_norm[:], scalar1=y_norm[:], scalar2=offset,
                     op0=ALU.mult, op1=ALU.add,
                 )
-
-        def collect_y():
-            nc.scalar.activation(
-                out=by_four(y_bc[:]), in_=bias_ps[0][:].rearrange("q t p -> q p t"),
-                func=ACT.Identity, scale=y_scale[:],
-            )
 
         w_grouped = keep.tile([P, D, PACK], BF16, name="w_grouped", align_bytes=64)
         w_codes = keep.tile([P, D], U32, name="w_codes", align_bytes=64)
@@ -364,6 +396,11 @@ def tile_hnnlayer_s_kernel(tc, h, weight, bias, gamma, beta, out):
                 out=u_grouped[i][:].bitcast(F32), in_=u_t[i][:].rearrange("p v r -> p r v")
             )
 
+        def regroup_u_on_vector(i):
+            nc.vector.tensor_copy(
+                out=u_grouped[i][:].bitcast(F32), in_=u_t[i][:].rearrange("p v r -> p r v")
+            )
+
         def multiply(i):
             nc.vector.quantize_mx(
                 out=u_codes[i][:].bitcast(FP8X4),
@@ -418,10 +455,10 @@ def tile_hnnlayer_s_kernel(tc, h, weight, bias, gamma, beta, out):
         sum_den = row_numbers("sum_den")
         sum_den_rsqrt = row_numbers("sum_den_rsqrt")
         r2_clip = row_numbers("r2_clip")
-        z_unit = row_numbers("z_unit")
+        half_unit = row_numbers("half_unit")
         ln_up2 = row_numbers("ln_up2")
         ln_dn2 = row_numbers("ln_dn2")
-        log_coef2 = row_numbers("log_coef2")
+        log_coef = row_numbers("log_coef")
 
         def moebius_1(rows):
             c = cols(rows)
@@ -473,16 +510,15 @@ def tile_hnnlayer_s_kernel(tc, h, weight, bias, gamma, beta, out):
             power(sum_den_rsqrt, sum_den, neg_half, rows)
 
         def norm_and_unit_of_r2(rows):
-            c = cols(rows)
             for i in rows:
                 nc.vector.tensor_scalar(
                     out=col(r2_clip, i), in0=col(sum_sq, i), scalar1=col(sum_den_rsqrt, i),
                     scalar2=BOUND, op0=ALU.mult, op1=ALU.min,
                 )
-            nc.vector.scalar_tensor_tensor(
-                out=z_unit[:, c], in0=r_sq_m1[:, c], scalar=-1.0, in1=sum_den_rsqrt[:, c],
-                op0=ALU.mult, op1=ALU.mult,
-            )
+                nc.vector.tensor_scalar(
+                    out=col(half_unit, i), in0=col(r_sq_m1, i), scalar1=-0.5,
+                    scalar2=col(sum_den_rsqrt, i), op0=ALU.mult, op1=ALU.mult,
+                )
 
         def log_of_r2(rows):
             c = cols(rows)
@@ -492,8 +528,8 @@ def tile_hnnlayer_s_kernel(tc, h, weight, bias, gamma, beta, out):
         def log_map_coefficient(rows):
             for i in rows:
                 nc.vector.tensor_scalar(
-                    out=col(log_coef2, i), in0=col(ln_up2, i), scalar1=col(ln_dn2, i),
-                    scalar2=col(z_unit, i), op0=ALU.subtract, op1=ALU.mult,
+                    out=col(log_coef, i), in0=col(ln_up2, i), scalar1=col(ln_dn2, i),
+                    scalar2=col(half_unit, i), op0=ALU.subtract, op1=ALU.mult,
                 )
 
         z = per_tile([P, D], F32, "z")
@@ -522,35 +558,30 @@ def tile_hnnlayer_s_kernel(tc, h, weight, bias, gamma, beta, out):
         def relu_square_sum_on_scalar(i):
             square_sum(relu_z[i][:], col(relu_sq, i))
 
-        v_norm2 = row_numbers("v_norm2")
-        v_rnorm2 = row_numbers("v_rnorm2")
         v_tanh = row_numbers("v_tanh")
+        relu_rnorm = row_numbers("relu_rnorm")
         out_coef = row_numbers("out_coef")
         result = per_tile([P, D], F32, "result")
 
         def norm_of_relu(rows):
             power(relu_norm, relu_sq, half, rows)
 
-        def norm_of_v(rows):
+        def tanh_of_v(rows):
             for i in rows:
-                nc.vector.tensor_scalar(
-                    out=col(v_norm2, i), in0=col(relu_norm, i), scalar1=NORM_MIN,
-                    scalar2=col(log_coef2, i), op0=ALU.max, op1=ALU.mult,
+                nc.scalar.activation(
+                    out=col(v_tanh, i), in_=col(relu_norm, i), func=ACT.Tanh,
+                    scale=col(log_coef, i),
                 )
 
-        def tanh_of_v(rows):
+        def reciprocal_of_relu(rows):
             c = cols(rows)
-            nc.scalar.activation(out=v_tanh[:, c], in_=v_norm2[:, c], func=ACT.Tanh, scale=0.5)
-
-        def reciprocal_of_v(rows):
-            c = cols(rows)
-            nc.vector.reciprocal(out=v_rnorm2[:, c], in_=v_norm2[:, c])
+            nc.vector.reciprocal(out=relu_rnorm[:, c], in_=relu_norm[:, c])
 
         def out_coefficient(rows):
             for i in rows:
                 nc.vector.tensor_scalar(
-                    out=col(out_coef, i), in0=col(v_tanh, i), scalar1=col(v_rnorm2, i),
-                    scalar2=col(log_coef2, i), op0=ALU.mult, op1=ALU.mult,
+                    out=col(out_coef, i), in0=col(relu_rnorm, i), scalar1=1.0 / NORM_MIN,
+                    scalar2=col(v_tanh, i), op0=ALU.min, op1=ALU.mult,
                 )
 
         def store(i):
@@ -572,16 +603,21 @@ def tile_hnnlayer_s_kernel(tc, h, weight, bias, gamma, beta, out):
         B = range(2, 4)
 
         spread(gamma_col, affine_ps[:, 0])
+        bias_square_sum()
         shifted_square_sum(0)
         shifted_sum(0)
         first_terms(A)
         shifted_square_sum(1)
         shifted_sum(1)
-        sums_of_h(0)
-        sums_of_h(1)
-        norm_of_h(0)
-        norm_of_h(1)
+        terms_of_h(0, nc.vector)
+        mean_of_h(0)
+        terms_of_h(1, nc.vector)
+        clip_of_h(0, nc.vector)
+        mean_of_h(1)
+        clip_of_h(1, nc.vector)
         root_of_h(A)
+        bias_clip()
+        bias_root()
         shifted_square_sum(2)
         shifted_sum(2)
         first_terms(B)
@@ -590,115 +626,106 @@ def tile_hnnlayer_s_kernel(tc, h, weight, bias, gamma, beta, out):
         shifted_square_sum(3)
         shifted_sum(3)
         spread(beta_col, affine_ps[:, 1])
-        bias_square_sum()
         transpose_weight(0)
         transpose_weight(1)
         spread_bias()
         log_of_h(A)
-        root_of_k(A)
-        sums_of_h(2)
-        sums_of_h(3)
-        norm_of_h(2)
-        norm_of_h(3)
+        terms_of_h(2, nc.gpsimd)
+        terms_of_h(3, nc.gpsimd)
+        clip_of_h(2, nc.gpsimd)
+        clip_of_h(3, nc.gpsimd)
         root_of_h(B)
-        bias_norm_steps()
+        mean_of_h(2)
+        mean_of_h(3)
+        root_of_k(A)
+        bias_exponential()
         deviation_of_h(2)
         deviation_of_h(3)
         regroup_weight(0)
-        regroup_weight(1)
         centre(0)
         centre(1)
-        layer_norm_factor(A)
         log_of_h(B)
+        layer_norm_factor(A)
         root_of_k(B)
-        layer_norm(0)
-        layer_norm(1)
-        bias_reciprocal()
-        square_sum_of_x(0)
-        square_sum_of_x(1)
-        norm_of_x(A)
-        load_table(ACT.Tanh, "warm_tanh_a", col(x_sq, 1))
+        bias_tanh()
         centre(2)
         centre(3)
+        regroup_weight(1)
+        layer_norm(0)
+        layer_norm(1)
         layer_norm_factor(B)
+        bias_reciprocal()
+        square_sum_of_x(0)
         layer_norm(2)
-        shrink_factor(A)
+        square_sum_of_x(1)
+        norm_of_x(A)
         layer_norm(3)
         square_sum_of_x(2)
         square_sum_of_x(3)
         norm_of_x(B)
-        bias_point()
+        load_table(ACT.Tanh, "warm_tanh_a", col(x_sq, 3))
+        quantise_weight()
+        scale_of_y()
+        shrink_factor(A)
         make_u(0)
         make_u(1)
-        regroup_u(0)
-        regroup_u(1)
-        collect_y()
-        quantise_weight()
-        multiply(0)
-        multiply(1)
         shrink_factor(B)
         make_u(2)
         make_u(3)
+        regroup_u(0)
+        regroup_u(1)
+        collect_y()
+        multiply(0)
+        multiply(1)
+        regroup_u_on_vector(2)
+        regroup_u_on_vector(3)
+        multiply(2)
+        multiply(3)
         bias_squares()
         square_sum_of_xt(0)
         square_sum_of_xt(1)
         norm_of_xt(A)
         dot_with_y(0)
-        regroup_u(2)
-        regroup_u(3)
-        multiply(2)
-        multiply(3)
-        dot_with_y(1)
-        tanh_of_norm(A)
-        moebius_1(A)
         square_sum_of_xt(2)
-        moebius_2(A)
+        dot_with_y(1)
         square_sum_of_xt(3)
         norm_of_xt(B)
-        moebius_3(A)
         dot_with_y(2)
-        moebius_4(A)
-        moebius_5(A)
-        dot_with_y(3)
-        moebius_6(A)
-        root_of_r2(A)
-        direction(0)
-        tanh_of_norm(B)
+        tanh_of_norm(ALL)
         load_table(ACT.Ln, "warm_ln_b", col(r_norm, 3))
-        moebius_1(B)
-        direction(1)
-        moebius_2(B)
-        relu_on_scalar(0)
-        relu_on_scalar(1)
-        moebius_3(B)
-        norm_and_unit_of_r2(A)
-        moebius_4(B)
-        moebius_5(B)
-        moebius_6(B)
+        dot_with_y(3)
+        moebius_1(ALL)
+        moebius_2(ALL)
+        moebius_3(ALL)
+        moebius_4(ALL)
+        moebius_5(ALL)
+        moebius_6(ALL)
+        root_of_r2(A)
         root_of_r2(B)
-        log_of_r2(A)
-        direction(2)
+        direction(0)
+        relu_on_scalar(0)
+        direction(1)
         relu_square_sum_on_scalar(0)
-        relu_square_sum_on_scalar(1)
-        direction(3)
+        norm_and_unit_of_r2(A)
+        direction(2)
         norm_and_unit_of_r2(B)
-        log_of_r2(B)
+        log_of_r2(ALL)
         load_table(ACT.Tanh, "warm_tanh_b", col(ln_dn2, 3))
+        relu_square_sum(1)
         norm_of_relu(A)
-        relu_square_sum(2)
+        direction(3)
         log_map_coefficient(A)
-        relu_square_sum(3)
-        norm_of_v(A)
         tanh_of_v(A)
-        norm_of_relu(B)
-        log_map_coefficient(B)
-        reciprocal_of_v(A)
+        relu_square_sum(2)
+        reciprocal_of_relu(A)
         out_coefficient(A)
-        finish(0)
-        norm_of_v(B)
-        tanh_of_v(B)
-        reciprocal_of_v(B)
+        relu_square_sum(3)
+        log_map_coefficient(B)
+        norm_of_relu(B)
+        finish_on_scalar(0)
         finish_on_scalar(1)
+        reciprocal_of_relu(B)
+        tanh_of_v(B)
         out_coefficient(B)
         finish(2)
-        finish(3)
+        finish_on_scalar(3)

@@ -384,6 +384,8 @@ def tile_hnnlayer_s_kernel(tc, h, weight, bias, gamma, beta, out):
 
         def make_u(i):
             nc.vector.tensor_scalar_mul(out=u[i][:], in0=x[i][:], scalar1=col(shrink, i))
+
+        def transpose_u(i):
             words = u[i][:].bitcast(F32)
             u_t[i] = psum_tr.tile([P, 2, P], F32, name="u_t", tag="tr")
             for v in range(2):
@@ -401,12 +403,14 @@ def tile_hnnlayer_s_kernel(tc, h, weight, bias, gamma, beta, out):
                 out=u_grouped[i][:].bitcast(F32), in_=u_t[i][:].rearrange("p v r -> p r v")
             )
 
-        def multiply(i):
+        def quantise_u(i):
             nc.vector.quantize_mx(
                 out=u_codes[i][:].bitcast(FP8X4),
                 scales=u_scales[i][:],
                 in_=u_grouped[i][:].rearrange("p r t -> p (r t)"),
             )
+
+        def multiply(i):
             nc.tensor.matmul_mx(
                 out=xt[i][:],
                 lhsT=u_codes[i][:].bitcast(FP8X4),
@@ -416,6 +420,18 @@ def tile_hnnlayer_s_kernel(tc, h, weight, bias, gamma, beta, out):
                 start=True,
                 stop=True,
             )
+
+        def keep_tensor_busy(passes):
+            for _ in range(passes):
+                nc.tensor.matmul_mx(
+                    out=xt[TILES - 1][:],
+                    lhsT=w_codes[:, 0:P].bitcast(FP8X4),
+                    lhsT_scale=w_scales[:, 0:P],
+                    rhs=w_codes[:].bitcast(FP8X4),
+                    rhs_scale=w_scales[:],
+                    start=True,
+                    stop=True,
+                )
 
         def square_sum_of_xt(i):
             squares = scrap.tile([P, D], BF16, name="squares")
@@ -618,6 +634,7 @@ def tile_hnnlayer_s_kernel(tc, h, weight, bias, gamma, beta, out):
         root_of_h(A)
         bias_clip()
         bias_root()
+        bias_exponential()
         shifted_square_sum(2)
         shifted_sum(2)
         first_terms(B)
@@ -630,15 +647,14 @@ def tile_hnnlayer_s_kernel(tc, h, weight, bias, gamma, beta, out):
         transpose_weight(1)
         spread_bias()
         log_of_h(A)
-        terms_of_h(2, nc.gpsimd)
-        terms_of_h(3, nc.gpsimd)
-        clip_of_h(2, nc.gpsimd)
-        clip_of_h(3, nc.gpsimd)
-        root_of_h(B)
+        terms_of_h(2, nc.vector)
+        terms_of_h(3, nc.vector)
         mean_of_h(2)
+        clip_of_h(2, nc.vector)
+        clip_of_h(3, nc.vector)
         mean_of_h(3)
+        root_of_h(B)
         root_of_k(A)
-        bias_exponential()
         deviation_of_h(2)
         deviation_of_h(3)
         regroup_weight(0)
@@ -665,21 +681,30 @@ def tile_hnnlayer_s_kernel(tc, h, weight, bias, gamma, beta, out):
         norm_of_x(B)
         load_table(ACT.Tanh, "warm_tanh_a", col(x_sq, 3))
         quantise_weight()
+        keep_tensor_busy(2)
         scale_of_y()
         shrink_factor(A)
         make_u(0)
+        transpose_u(0)
         make_u(1)
+        transpose_u(1)
         shrink_factor(B)
         make_u(2)
+        transpose_u(2)
         make_u(3)
         regroup_u(0)
+        quantise_u(0)
+        multiply(0)
+        transpose_u(3)
         regroup_u(1)
         collect_y()
-        multiply(0)
+        quantise_u(1)
         multiply(1)
         regroup_u_on_vector(2)
         regroup_u_on_vector(3)
+        quantise_u(2)
         multiply(2)
+        quantise_u(3)
         multiply(3)
         bias_squares()
         square_sum_of_xt(0)
@@ -718,14 +743,14 @@ def tile_hnnlayer_s_kernel(tc, h, weight, bias, gamma, beta, out):
         tanh_of_v(A)
         relu_square_sum(2)
         reciprocal_of_relu(A)
-        out_coefficient(A)
         relu_square_sum(3)
-        log_map_coefficient(B)
         norm_of_relu(B)
-        finish_on_scalar(0)
+        out_coefficient(A)
+        log_map_coefficient(B)
+        finish(0)
         finish_on_scalar(1)
-        reciprocal_of_relu(B)
         tanh_of_v(B)
+        reciprocal_of_relu(B)
         out_coefficient(B)
         finish(2)
         finish_on_scalar(3)

@@ -81,18 +81,16 @@ def tile_hnnlayer_s_kernel(tc, h, weight, bias, gamma, beta, out):
         h_sb = keep.tile([P, TILES, D], BF16, name="h_sb")
         for i in range(TILES):
             nc.sync.dma_start(out=h_sb[:, i, :], in_=h[i * P : (i + 1) * P, :])
-        nc.sync.dma_start(out=bias_col[:], in_=bias.rearrange("o (p t) -> p (o t)", t=PACK))
-        nc.sync.dma_start(out=beta_col[:], in_=beta.rearrange("(p t) -> p t", t=PACK))
         w_sb = keep.tile([P, TILES, D], BF16, name="w_sb")
         nc.sync.dma_start(out=w_sb[:], in_=weight.rearrange("(o p) k -> p o k", p=P))
+        nc.sync.dma_start(out=beta_col[:], in_=beta.rearrange("(p t) -> p t", t=PACK))
+        nc.sync.dma_start(out=bias_col[:], in_=bias.rearrange("o (p t) -> p (o t)", t=PACK))
         half = row_numbers("half")
         nc.vector.memset(half[:], 0.5)
         neg_half = row_numbers("neg_half")
         nc.vector.memset(neg_half[:], -0.5)
         ones = one_number("ones")
         nc.vector.memset(ones[:], 1.0)
-        neg_one = one_number("neg_one")
-        nc.vector.memset(neg_one[:], -1.0)
         two = one_number("two")
         nc.vector.memset(two[:], 2.0)
         tiny = one_number("tiny")
@@ -151,7 +149,10 @@ def tile_hnnlayer_s_kernel(tc, h, weight, bias, gamma, beta, out):
 
         def first_terms(rows):
             c = cols(rows)
-            nc.vector.tensor_scalar_mul(out=first_x2[:, c], in0=first[:, c], scalar1=2.0)
+            nc.gpsimd.tensor_scalar(
+                out=first_x2[:, c], in0=first[:, c], scalar1=2.0, scalar2=0.0,
+                op0=ALU.mult, op1=ALU.add,
+            )
             nc.scalar.activation(
                 out=first_sq[:, c], in_=first[:, c], func=ACT.Square, scale=math.sqrt(D),
                 bias=tiny[:],
@@ -302,16 +303,18 @@ def tile_hnnlayer_s_kernel(tc, h, weight, bias, gamma, beta, out):
         def bias_exponential():
             gpsimd_power(bias_exp, two[:], bias_log2[:])
 
-        def bias_tanh():
-            nc.gpsimd.tensor_scalar_add(out=bias_exp_p1[:], in0=bias_exp[:], scalar1=1.0)
-            gpsimd_power(bias_rexp, bias_exp_p1[:], neg_one[:])
-            nc.gpsimd.tensor_scalar(
+        def bias_tanh_1():
+            nc.vector.tensor_scalar_add(out=bias_exp_p1[:], in0=bias_exp[:], scalar1=1.0)
+            nc.vector.reciprocal(out=bias_rlog2[:], in_=bias_log2[:])
+
+        def bias_tanh_2():
+            nc.vector.reciprocal(out=bias_rexp[:], in_=bias_exp_p1[:])
+
+        def bias_tanh_3():
+            nc.vector.tensor_scalar(
                 out=y_norm[:], in0=bias_rexp[:], scalar1=-2.0, scalar2=1.0,
                 op0=ALU.mult, op1=ALU.add,
             )
-
-        def bias_reciprocal():
-            nc.vector.reciprocal(out=bias_rlog2[:], in_=bias_log2[:])
 
         def scale_of_y():
             nc.vector.tensor_scalar(
@@ -387,7 +390,11 @@ def tile_hnnlayer_s_kernel(tc, h, weight, bias, gamma, beta, out):
 
         def transpose_u(i):
             words = u[i][:].bitcast(F32)
-            u_t[i] = psum_tr.tile([P, 2, P], F32, name="u_t", tag="tr")
+            if i < 2:
+                u_t[i] = psum_tr.tile([P, 2, P], F32, name="u_t", tag="tr")[:]
+            else:
+                half_bank = xt[TILES - 1][:, (i - 2) * 2 * P : (i - 1) * 2 * P]
+                u_t[i] = half_bank.rearrange("p (v r) -> p v r", v=2)
             for v in range(2):
                 nc.tensor.transpose(
                     out=u_t[i][:, v, :], in_=words[:, v : D // 2 : 2], identity=ident_words[:]
@@ -395,12 +402,12 @@ def tile_hnnlayer_s_kernel(tc, h, weight, bias, gamma, beta, out):
 
         def regroup_u(i):
             nc.scalar.copy(
-                out=u_grouped[i][:].bitcast(F32), in_=u_t[i][:].rearrange("p v r -> p r v")
+                out=u_grouped[i][:].bitcast(F32), in_=u_t[i].rearrange("p v r -> p r v")
             )
 
         def regroup_u_on_vector(i):
             nc.vector.tensor_copy(
-                out=u_grouped[i][:].bitcast(F32), in_=u_t[i][:].rearrange("p v r -> p r v")
+                out=u_grouped[i][:].bitcast(F32), in_=u_t[i].rearrange("p v r -> p r v")
             )
 
         def quantise_u(i):
@@ -424,7 +431,7 @@ def tile_hnnlayer_s_kernel(tc, h, weight, bias, gamma, beta, out):
         def keep_tensor_busy(passes):
             for _ in range(passes):
                 nc.tensor.matmul_mx(
-                    out=xt[TILES - 1][:],
+                    out=xt[2][:],
                     lhsT=w_codes[:, 0:P].bitcast(FP8X4),
                     lhsT_scale=w_scales[:, 0:P],
                     rhs=w_codes[:].bitcast(FP8X4),
@@ -496,23 +503,23 @@ def tile_hnnlayer_s_kernel(tc, h, weight, bias, gamma, beta, out):
         def moebius_4(rows):
             c = cols(rows)
             nc.vector.scalar_tensor_tensor(
-                out=xt_coef[:, c], in0=r_y2[:, c], scalar=y_sq_p1[:], in1=rho[:, c],
-                op0=ALU.add, op1=ALU.mult,
-            )
-            nc.vector.scalar_tensor_tensor(
                 out=sum_sq[:, c], in0=r_sq[:, c], scalar=y_sq[:], in1=r_y2[:, c],
                 op0=ALU.add, op1=ALU.add,
+            )
+            nc.vector.scalar_tensor_tensor(
+                out=xt_coef[:, c], in0=r_y2[:, c], scalar=y_sq_p1[:], in1=rho[:, c],
+                op0=ALU.add, op1=ALU.mult,
             )
 
         def moebius_5(rows):
             c = cols(rows)
             nc.vector.scalar_tensor_tensor(
-                out=xt_share[:, c], in0=xt_coef[:, c], scalar=-1.0, in1=r_sq_rm1[:, c],
-                op0=ALU.mult, op1=ALU.mult,
-            )
-            nc.vector.scalar_tensor_tensor(
                 out=den[:, c], in0=r_sq_m1[:, c], scalar=y_sq_m1[:], in1=sum_sq[:, c],
                 op0=ALU.mult, op1=ALU.add,
+            )
+            nc.vector.scalar_tensor_tensor(
+                out=xt_share[:, c], in0=xt_coef[:, c], scalar=-1.0, in1=r_sq_rm1[:, c],
+                op0=ALU.mult, op1=ALU.mult,
             )
 
         def moebius_6(rows):
@@ -619,10 +626,10 @@ def tile_hnnlayer_s_kernel(tc, h, weight, bias, gamma, beta, out):
         B = range(2, 4)
 
         spread(gamma_col, affine_ps[:, 0])
-        bias_square_sum()
         shifted_square_sum(0)
         shifted_sum(0)
         first_terms(A)
+        first_terms(B)
         shifted_square_sum(1)
         shifted_sum(1)
         terms_of_h(0, nc.vector)
@@ -632,19 +639,16 @@ def tile_hnnlayer_s_kernel(tc, h, weight, bias, gamma, beta, out):
         mean_of_h(1)
         clip_of_h(1, nc.vector)
         root_of_h(A)
-        bias_clip()
-        bias_root()
-        bias_exponential()
         shifted_square_sum(2)
         shifted_sum(2)
-        first_terms(B)
         deviation_of_h(0)
         deviation_of_h(1)
         shifted_square_sum(3)
         shifted_sum(3)
-        spread(beta_col, affine_ps[:, 1])
         transpose_weight(0)
         transpose_weight(1)
+        spread(beta_col, affine_ps[:, 1])
+        bias_square_sum()
         spread_bias()
         log_of_h(A)
         terms_of_h(2, nc.vector)
@@ -660,42 +664,45 @@ def tile_hnnlayer_s_kernel(tc, h, weight, bias, gamma, beta, out):
         regroup_weight(0)
         centre(0)
         centre(1)
+        bias_clip()
         log_of_h(B)
         layer_norm_factor(A)
         root_of_k(B)
-        bias_tanh()
+        bias_root()
+        bias_exponential()
         centre(2)
         centre(3)
         regroup_weight(1)
         layer_norm(0)
         layer_norm(1)
         layer_norm_factor(B)
-        bias_reciprocal()
         square_sum_of_x(0)
         layer_norm(2)
+        bias_tanh_1()
         square_sum_of_x(1)
         norm_of_x(A)
         layer_norm(3)
+        bias_tanh_2()
         square_sum_of_x(2)
         square_sum_of_x(3)
         norm_of_x(B)
         load_table(ACT.Tanh, "warm_tanh_a", col(x_sq, 3))
         quantise_weight()
-        keep_tensor_busy(2)
-        scale_of_y()
+        bias_tanh_3()
         shrink_factor(A)
         make_u(0)
         transpose_u(0)
         make_u(1)
+        scale_of_y()
         transpose_u(1)
         shrink_factor(B)
         make_u(2)
         transpose_u(2)
         make_u(3)
+        transpose_u(3)
         regroup_u(0)
         quantise_u(0)
         multiply(0)
-        transpose_u(3)
         regroup_u(1)
         collect_y()
         quantise_u(1)

@@ -81,9 +81,9 @@ def tile_hnnlayer_s_kernel(tc, h, weight, bias, gamma, beta, out):
         h_sb = keep.tile([P, TILES, D], BF16, name="h_sb")
         for i in range(TILES):
             nc.sync.dma_start(out=h_sb[:, i, :], in_=h[i * P : (i + 1) * P, :])
+        nc.sync.dma_start(out=beta_col[:], in_=beta.rearrange("(p t) -> p t", t=PACK))
         w_sb = keep.tile([P, TILES, D], BF16, name="w_sb")
         nc.sync.dma_start(out=w_sb[:], in_=weight.rearrange("(o p) k -> p o k", p=P))
-        nc.sync.dma_start(out=beta_col[:], in_=beta.rearrange("(p t) -> p t", t=PACK))
         nc.sync.dma_start(out=bias_col[:], in_=bias.rearrange("o (p t) -> p (o t)", t=PACK))
         half = row_numbers("half")
         nc.vector.memset(half[:], 0.5)
@@ -645,9 +645,9 @@ def tile_hnnlayer_s_kernel(tc, h, weight, bias, gamma, beta, out):
         deviation_of_h(1)
         shifted_square_sum(3)
         shifted_sum(3)
+        spread(beta_col, affine_ps[:, 1])
         transpose_weight(0)
         transpose_weight(1)
-        spread(beta_col, affine_ps[:, 1])
         bias_square_sum()
         spread_bias()
         log_of_h(A)
@@ -678,18 +678,18 @@ def tile_hnnlayer_s_kernel(tc, h, weight, bias, gamma, beta, out):
         layer_norm_factor(B)
         square_sum_of_x(0)
         layer_norm(2)
-        bias_tanh_1()
         square_sum_of_x(1)
         norm_of_x(A)
         layer_norm(3)
-        bias_tanh_2()
+        bias_tanh_1()
         square_sum_of_x(2)
         square_sum_of_x(3)
         norm_of_x(B)
         load_table(ACT.Tanh, "warm_tanh_a", col(x_sq, 3))
         quantise_weight()
-        bias_tanh_3()
+        bias_tanh_2()
         shrink_factor(A)
+        bias_tanh_3()
         make_u(0)
         transpose_u(0)
         make_u(1)

import math
from contextlib import ExitStack

import concourse.mybir as mybir
from concourse.masks import make_identity

F32 = mybir.dt.float32
BF16 = mybir.dt.bfloat16
U32 = mybir.dt.uint32
U8 = mybir.dt.uint8
FP8X4 = mybir.dt.float8_e4m3fn_x4
ALU = mybir.AluOpType
ACT = mybir.ActivationFunctionType

P = 128
PACK = 4
N_ROWS = 512
D = 512
TILES = N_ROWS // P

BOUND = 1.0 - 168.0 * 2.0 ** -24
ARTANH_BOUND = 0.5 * math.log((1.0 + BOUND) / (1.0 - BOUND))
LN_EPS = 1e-5
DEV_SCALE = 0.25 / (D * LN_EPS)
K_SCALE = 0.5 / math.sqrt(LN_EPS)
TWO_LOG2E = 2.0 / math.log(2.0)
NORM_MIN = 1e-15
NORM_MIN_SQ = 1e-30
SUM_SQ_MIN = 1e-20
R_SQ_MAX = 1.0 - 2.0 ** -24

FLOPS = 2 * N_ROWS * D * D


def tile_hnnlayer_s_kernel(tc, h, weight, bias, gamma, beta, out):
    nc = tc.nc
    with ExitStack() as ctx:
        keep = ctx.enter_context(tc.tile_pool(name="keep", bufs=1))
        scrap = ctx.enter_context(tc.tile_pool(name="scrap", bufs=4))
        psum_tr = ctx.enter_context(tc.psum_pool(name="psum_tr", bufs=3))
        psum_keep = ctx.enter_context(tc.psum_pool(name="psum_keep", bufs=1))
        ctx.enter_context(tc.manual_schedule())

        def per_tile(shape, dtype, name):
            return [
                keep.tile(shape, dtype, name="%s%d" % (name, i), align_bytes=64)
                for i in range(TILES)
            ]

        def row_numbers(name):
            return keep.tile([P, TILES], F32, name=name)

        def one_number(name):
            return keep.tile([P, 1], F32, name=name)

        def cols(rows):
            return slice(rows[0], rows[-1] + 1)

        def col(numbers, i):
            return numbers[:, i : i + 1]

        def by_four(features):
            return features.rearrange("q (p t) -> q p t", t=PACK)

        def power(dst, src, exponent, rows):
            c = cols(rows)
            nc.gpsimd.tensor_tensor(out=dst[:, c], in0=src[:, c], in1=exponent[:, c], op=ALU.pow)

        def load_table(func, name, source):
            unused = one_number(name)
            nc.scalar.activation(out=unused[:], in_=source, func=func)

        def square_sum(src, total):
            squares = scrap.tile([P, D], BF16, name="squares")
            nc.scalar.activation(out=squares[:], in_=src, func=ACT.Square, accum_out=total)

        gamma_col = keep.tile([P, PACK], BF16, name="gamma_col")
        beta_col = keep.tile([P, PACK], BF16, name="beta_col")
        bias_col = keep.tile([P, PACK], BF16, name="bias_col")
        nc.scalar.dma_start(out=gamma_col[:], in_=gamma.rearrange("(p t) -> p t", t=PACK))
        h_sb = keep.tile([P, TILES, D], BF16, name="h_sb")
        for i in range(TILES):
            nc.sync.dma_start(out=h_sb[:, i, :], in_=h[i * P : (i + 1) * P, :])
        nc.sync.dma_start(out=beta_col[:], in_=beta.rearrange("(p t) -> p t", t=PACK))
        w_sb = keep.tile([P, TILES, D], BF16, name="w_sb")
        nc.sync.dma_start(out=w_sb[:], in_=weight.rearrange("(o p) k -> p o k", p=P))
        nc.sync.dma_start(out=bias_col[:], in_=bias.rearrange("o (p t) -> p (o t)", t=PACK))
        half = row_numbers("half")
        nc.vector.memset(half[:], 0.5)
        neg_half = row_numbers("neg_half")
        nc.vector.memset(neg_half[:], -0.5)
        ones = one_number("ones")
        nc.vector.memset(ones[:], 1.0)
        two = one_number("two")
        nc.vector.memset(two[:], 2.0)
        tiny = one_number("tiny")
        nc.vector.memset(tiny[:], 2.0 ** -53)
        ident = keep.tile([P, P], BF16, name="ident")
        make_identity(nc, ident[:])
        ident_words = keep.tile([P, P], F32, name="ident_words")
        make_identity(nc, ident_words[:])
        load_table(ACT.Ln, "warm_ln", ones[:])

        affine_ps = psum_keep.tile([P, 2, PACK, P], BF16, name="affine_ps")
        bias_ps = []
        gamma_bc = affine_ps[:, 0].rearrange("q t p -> q p t")
        beta_bc = affine_ps[:, 1].rearrange("q t p -> q p t")

        def spread(vec_col, rows_ps):
            for t in range(PACK):
                nc.tensor.transpose(
                    out=rows_ps[:, t, :],
                    in_=vec_col[:, t : t + 1].to_broadcast([P, P]),
                    identity=ident[:],
                )

        def spread_bias():
            rows_ps = psum_tr.tile([P, PACK, P], BF16, name="bias_ps", tag="tr")
            spread(bias_col, rows_ps)
            bias_ps.append(rows_ps)

        first = h_sb[:, :, 0]
        d_sum = row_numbers("d_sum")
        d_sq = row_numbers("d_sq")

        def shifted_sum(i):
            shifted = scrap.tile([P, D], F32, name="shifted")
            nc.vector.tensor_scalar(
                out=shifted[:], in0=h_sb[:, i, :], scalar1=h_sb[:, i, 0:1], scalar2=None,
                op0=ALU.subtract, op1=ALU.add, accum_out=col(d_sum, i),
            )

        def shifted_square_sum(i):
            squares = scrap.tile([P, D], BF16, name="squares")
            nc.scalar.activation(
                out=squares[:], in_=h_sb[:, i, :], func=ACT.Square, scale=-1.0,
                bias=h_sb[:, i, 0:1], accum_out=col(d_sq, i),
            )

        mean = row_numbers("mean")
        first_x2 = row_numbers("first_x2")
        first_sq = row_numbers("first_sq")
        h_sq_b = [keep.tile([P, 2], F32, name="h_sq_b%d" % pair) for pair in range(2)]
        h_sq_clip = [keep.tile([P, 2], F32, name="h_sq_clip%d" % pair) for pair in range(2)]
        neg_sum_sq = row_numbers("neg_sum_sq")
        dev_sq = row_numbers("dev_sq")
        h_sq = row_numbers("h_sq")
        h_clip = row_numbers("h_clip")

        def first_terms(rows):
            c = cols(rows)
            nc.gpsimd.tensor_scalar(
                out=first_x2[:, c], in0=first[:, c], scalar1=2.0, scalar2=0.0,
                op0=ALU.mult, op1=ALU.add,
            )
            nc.scalar.activation(
                out=first_sq[:, c], in_=first[:, c], func=ACT.Square, scale=math.sqrt(D),
                bias=tiny[:],
            )

        def mean_of_h(i):
            nc.vector.tensor_scalar(
                out=col(mean, i), in0=col(d_sum, i), scalar1=1.0 / D, scalar2=h_sb[:, i, 0:1],
                op0=ALU.mult, op1=ALU.add,
            )
            nc.vector.tensor_scalar(
                out=col(neg_sum_sq, i), in0=col(d_sum, i), scalar1=-DEV_SCALE / D,
                scalar2=col(d_sum, i), op0=ALU.mult, op1=ALU.mult,
            )

        def terms_of_h(i, engine):
            engine.tensor_scalar(
                out=col(h_sq_b[i // 2], i % 2), in0=col(d_sum, i), scalar1=col(first_x2, i),
                scalar2=col(first_sq, i), op0=ALU.mult, op1=ALU.add,
            )

        def clip_of_h(i, engine):
            engine.tensor_scalar(
                out=col(h_sq_clip[i // 2], i % 2), in0=col(h_sq_b[i // 2], i % 2),
                scalar1=col(d_sq, i), scalar2=BOUND * BOUND, op0=ALU.add, op1=ALU.min,
            )

        def deviation_of_h(i):
            nc.scalar.activation(
                out=col(h_sq, i), in_=col(d_sq, i), func=ACT.Identity, scale=1.0,
                bias=col(h_sq_b[i // 2], i % 2),
            )
            nc.scalar.activation(
                out=col(dev_sq, i), in_=col(d_sq, i), func=ACT.Identity, scale=DEV_SCALE,
                bias=col(neg_sum_sq, i),
            )

        def root_of_h(rows):
            c = cols(rows)
            nc.gpsimd.tensor_tensor(
                out=h_clip[:, c], in0=h_sq_clip[rows[0] // 2][:], in1=half[:, c], op=ALU.pow
            )

        centred = per_tile([P, D], F32, "centred")

        def centre(i):
            nc.vector.scalar_tensor_tensor(
                out=by_four(centred[i][:]), in0=by_four(h_sb[:, i, :]), scalar=col(mean, i),
                in1=gamma_bc, op0=ALU.subtract, op1=ALU.mult,
            )

        ln_up = row_numbers("ln_up")
        ln_dn = row_numbers("ln_dn")
        theta_sq = row_numbers("theta_sq")
        ln_up_scaled = row_numbers("ln_up_scaled")
        theta2 = row_numbers("theta2")
        k_arg = row_numbers("k_arg")
        k_rsqrt = row_numbers("k_rsqrt")
        k = row_numbers("k")

        def log_of_h(rows):
            c = cols(rows)
            nc.scalar.activation(out=ln_up[:, c], in_=h_clip[:, c], func=ACT.Ln, bias=1.0, scale=1.0)
            nc.scalar.activation(out=ln_dn[:, c], in_=h_clip[:, c], func=ACT.Ln, bias=1.0, scale=-1.0)
            for i in rows:
                nc.scalar.activation(
                    out=col(theta_sq, i), in_=col(ln_dn, i), func=ACT.Square,
                    scale=-1.0, bias=col(ln_up, i),
                )
            nc.scalar.activation(
                out=ln_up_scaled[:, c], in_=ln_up[:, c], func=ACT.Identity, scale=K_SCALE
            )
            for i in rows:
                nc.scalar.activation(
                    out=col(k_arg, i), in_=col(theta_sq, i), func=ACT.Identity,
                    scale=col(dev_sq, i), bias=col(h_sq, i),
                )
            for i in rows:
                nc.scalar.activation(
                    out=col(theta2, i), in_=col(ln_dn, i), func=ACT.Identity,
                    scale=-K_SCALE, bias=col(ln_up_scaled, i),
                )

        def root_of_k(rows):
            power(k_rsqrt, k_arg, neg_half, rows)

        def layer_norm_factor(rows):
            for i in rows:
                nc.scalar.activation(
                    out=col(k, i), in_=col(k_rsqrt, i), func=ACT.Identity, scale=col(theta2, i)
                )

        x = per_tile([P, D], F32, "x")
        x_sq = row_numbers("x_sq")
        x_rnorm = row_numbers("x_rnorm")

        def layer_norm(i):
            nc.vector.scalar_tensor_tensor(
                out=by_four(x[i][:]), in0=by_four(centred[i][:]), scalar=col(k, i), in1=beta_bc,
                op0=ALU.mult, op1=ALU.add,
            )

        def square_sum_of_x(i):
            square_sum(x[i][:], col(x_sq, i))

        def square_sum_of_x_on_vector(i):
            products = scrap.tile([P, D], F32, name="products")
            nc.vector.scalar_tensor_tensor(
                out=products[:], in0=x[i][:], scalar=1.0, in1=x[i][:],
                op0=ALU.mult, op1=ALU.mult, accum_out=col(x_sq, i),
            )

        bias_sq_clip = one_number("bias_sq_clip")
        bias_log2 = one_number("bias_log2")
        bias_rlog2 = one_number("bias_rlog2")
        bias_exp = one_number("bias_exp")
        bias_exp_p1 = one_number("bias_exp_p1")
        bias_rexp = one_number("bias_rexp")
        y_norm = one_number("y_norm")
        y_scale = one_number("y_scale")
        y_sq = one_number("y_sq")
        y_sq_p1 = one_number("y_sq_p1")
        y_sq_m1 = one_number("y_sq_m1")
        y_bc = keep.tile([P, D], F32, name="y_bc")

        def bias_square_sum():
            for t in range(PACK):
                nc.tensor.matmul(
                    out=xt[0][:, 0:1],
                    lhsT=bias_col[:, t : t + 1].to_broadcast([P, P]),
                    rhs=bias_col[:, t : t + 1],
                    start=(t == 0),
                    stop=(t == PACK - 1),
                )

        def bias_clip():
            nc.vector.tensor_scalar(
                out=bias_sq_clip[:], in0=xt[0][:, 0:1], scalar1=NORM_MIN_SQ,
                scalar2=TWO_LOG2E * TWO_LOG2E, op0=ALU.max, op1=ALU.mult,
            )

        def gpsimd_power(dst, base, exponent):
            nc.gpsimd.tensor_tensor(out=dst[:], in0=base, in1=exponent, op=ALU.pow)

        def bias_root():
            gpsimd_power(bias_log2, bias_sq_clip[:], half[:, 0:1])

        def bias_exponential():
            gpsimd_power(bias_exp, two[:], bias_log2[:])

        def bias_tanh_1():
            nc.vector.tensor_scalar_add(out=bias_exp_p1[:], in0=bias_exp[:], scalar1=1.0)
            nc.vector.reciprocal(out=bias_rlog2[:], in_=bias_log2[:])

        def bias_tanh_2():
            nc.vector.reciprocal(out=bias_rexp[:], in_=bias_exp_p1[:])

        def bias_tanh_3():
            nc.vector.tensor_scalar(
                out=y_norm[:], in0=bias_rexp[:], scalar1=-2.0, scalar2=1.0,
                op0=ALU.mult, op1=ALU.add,
            )

        def scale_of_y():
            nc.vector.tensor_scalar(
                out=y_scale[:], in0=y_norm[:], scalar1=bias_rlog2[:], scalar2=TWO_LOG2E,
                op0=ALU.mult, op1=ALU.mult,
            )

        def collect_y():
            nc.scalar.activation(
                out=by_four(y_bc[:]), in_=bias_ps[0][:].rearrange("q t p -> q p t"),
                func=ACT.Identity, scale=y_scale[:],
            )

        def bias_squares():
            nc.vector.tensor_scalar_mul(out=y_sq[:], in0=y_norm[:], scalar1=y_norm[:])
            for total, offset in ((y_sq_p1, 1.0), (y_sq_m1, -1.0)):
                nc.vector.tensor_scalar(
                    out=total[:], in0=y_norm[:], scalar1=y_norm[:], scalar2=offset,
                    op0=ALU.mult, op1=ALU.add,
                )

        w_grouped = keep.tile([P, D, PACK], BF16, name="w_grouped", align_bytes=64)
        w_codes = keep.tile([P, D], U32, name="w_codes", align_bytes=64)
        w_scales = keep.tile([P, D], U8, name="w_scales", align_bytes=64)
        w_t = {}

        def transpose_weight(b):
            w_t[b] = psum_tr.tile([P, 2, 2, P], F32, name="w_t", tag="tr")
            for a in range(2):
                words = w_sb[:, 2 * b + a, :].bitcast(F32)
                for v in range(2):
                    nc.tensor.transpose(
                        out=w_t[b][:, a, v, :], in_=words[:, v : D // 2 : 2], identity=ident_words[:]
                    )

        def regroup_weight(b):
            nc.scalar.copy(
                out=w_grouped[:, 2 * b * P : 2 * (b + 1) * P, :].bitcast(F32).rearrange(
                    "p (a r) v -> p a r v", a=2
                ),
                in_=w_t[b][:].rearrange("p a v r -> p a r v"),
            )

        def quantise_weight():
            nc.vector.quantize_mx(
                out=w_codes[:].bitcast(FP8X4),
                scales=w_scales[:],
                in_=w_grouped[:].rearrange("p c t -> p (c t)"),
            )

        shrink = row_numbers("shrink")
        u = per_tile([P, D], BF16, "u")
        u_t = {}
        u_grouped = per_tile([P, P, PACK], BF16, "u_grouped")
        u_codes = per_tile([P, P], U32, "u_codes")
        u_scales = per_tile([P, P], U8, "u_scales")
        xt = [psum_keep.tile([P, D], F32, name="xt%d" % i) for i in range(TILES)]
        xt_sq = row_numbers("xt_sq")
        xt_y2 = row_numbers("xt_y2")

        def norm_of_x(rows):
            power(x_rnorm, x_sq, neg_half, rows)

        def shrink_factor(rows):
            c = cols(rows)
            nc.vector.tensor_scalar(
                out=shrink[:, c], in0=x_rnorm[:, c], scalar1=ARTANH_BOUND, scalar2=1.0,
                op0=ALU.mult, op1=ALU.min,
            )

        def make_u(i):
            nc.vector.tensor_scalar_mul(out=u[i][:], in0=x[i][:], scalar1=col(shrink, i))

        def transpose_u(i):
            words = u[i][:].bitcast(F32)
            if i < 2:
                u_t[i] = psum_tr.tile([P, 2, P], F32, name="u_t", tag="tr")[:]
            else:
                half_bank = xt[TILES - 1][:, (i - 2) * 2 * P : (i - 1) * 2 * P]
                u_t[i] = half_bank.rearrange("p (v r) -> p v r", v=2)
            for v in range(2):
                nc.tensor.transpose(
                    out=u_t[i][:, v, :], in_=words[:, v : D // 2 : 2], identity=ident_words[:]
                )

        def regroup_u(i):
            nc.scalar.copy(
                out=u_grouped[i][:].bitcast(F32), in_=u_t[i].rearrange("p v r -> p r v")
            )

        def regroup_u_on_vector(i):
            nc.vector.tensor_copy(
                out=u_grouped[i][:].bitcast(F32), in_=u_t[i].rearrange("p v r -> p r v")
            )

        def quantise_u(i):
            nc.vector.quantize_mx(
                out=u_codes[i][:].bitcast(FP8X4),
                scales=u_scales[i][:],
                in_=u_grouped[i][:].rearrange("p r t -> p (r t)"),
            )

        def multiply(i):
            nc.tensor.matmul_mx(
                out=xt[i][:],
                lhsT=u_codes[i][:].bitcast(FP8X4),
                lhsT_scale=u_scales[i][:],
                rhs=w_codes[:].bitcast(FP8X4),
                rhs_scale=w_scales[:],
                start=True,
                stop=True,
            )

        def keep_tensor_busy(passes):
            for _ in range(passes):
                nc.tensor.matmul_mx(
                    out=xt[2][:],
                    lhsT=w_codes[:, 0:P].bitcast(FP8X4),
                    lhsT_scale=w_scales[:, 0:P],
                    rhs=w_codes[:].bitcast(FP8X4),
                    rhs_scale=w_scales[:],
                    start=True,
                    stop=True,
                )

        def square_sum_of_xt(i):
            squares = scrap.tile([P, D], BF16, name="squares")
            nc.scalar.activation(
                out=squares[:], in_=xt[i][:], func=ACT.Square, bias=tiny[:],
                accum_out=col(xt_sq, i),
            )

        def dot_with_y(i):
            products = scrap.tile([P, D], F32, name="products")
            nc.vector.scalar_tensor_tensor(
                out=products[:], in0=xt[i][:], scalar=2.0, in1=y_bc[:],
                op0=ALU.mult, op1=ALU.mult, accum_out=col(xt_y2, i),
            )

        xt_norm = row_numbers("xt_norm")
        r_norm = row_numbers("r_norm")
        xt_rnorm = row_numbers("xt_rnorm")

        def norm_of_xt(rows):
            power(xt_norm, xt_sq, half, rows)

        def tanh_of_norm(rows):
            c = cols(rows)
            nc.scalar.activation(out=r_norm[:, c], in_=xt_norm[:, c], func=ACT.Tanh)
            nc.scalar.activation(out=r_sq[:, c], in_=r_norm[:, c], func=ACT.Square)

        r_y2 = row_numbers("r_y2")
        rho = row_numbers("rho")
        r_sq = row_numbers("r_sq")
        r_sq_m1 = row_numbers("r_sq_m1")
        r_sq_rm1 = row_numbers("r_sq_rm1")
        xt_coef = row_numbers("xt_coef")
        xt_share = row_numbers("xt_share")
        den = row_numbers("den")
        sum_sq = row_numbers("sum_sq")
        sum_den = row_numbers("sum_den")
        sum_den_rsqrt = row_numbers("sum_den_rsqrt")
        r2_clip = row_numbers("r2_clip")
        half_unit = row_numbers("half_unit")
        ln_up2 = row_numbers("ln_up2")
        ln_dn2 = row_numbers("ln_dn2")
        log_coef = row_numbers("log_coef")

        def moebius_1(rows):
            c = cols(rows)
            nc.vector.reciprocal(out=xt_rnorm[:, c], in_=xt_norm[:, c])

        def moebius_2(rows):
            c = cols(rows)
            nc.vector.tensor_mul(out=rho[:, c], in0=r_norm[:, c], in1=xt_rnorm[:, c])
            nc.vector.tensor_scalar(
                out=r_sq_m1[:, c], in0=r_sq[:, c], scalar1=R_SQ_MAX, scalar2=-1.0,
                op0=ALU.min, op1=ALU.add,
            )

        def moebius_3(rows):
            c = cols(rows)
            nc.vector.tensor_mul(out=r_y2[:, c], in0=rho[:, c], in1=xt_y2[:, c])
            nc.vector.reciprocal(out=r_sq_rm1[:, c], in_=r_sq_m1[:, c])

        def moebius_4(rows):
            c = cols(rows)
            nc.vector.scalar_tensor_tensor(
                out=sum_sq[:, c], in0=r_sq[:, c], scalar=y_sq[:], in1=r_y2[:, c],
                op0=ALU.add, op1=ALU.add,
            )
            nc.vector.scalar_tensor_tensor(
                out=xt_coef[:, c], in0=r_y2[:, c], scalar=y_sq_p1[:], in1=rho[:, c],
                op0=ALU.add, op1=ALU.mult,
            )

        def moebius_5(rows):
            c = cols(rows)
            nc.vector.scalar_tensor_tensor(
                out=den[:, c], in0=r_sq_m1[:, c], scalar=y_sq_m1[:], in1=sum_sq[:, c],
                op0=ALU.mult, op1=ALU.add,
            )
            nc.vector.scalar_tensor_tensor(
                out=xt_share[:, c], in0=xt_coef[:, c], scalar=-1.0, in1=r_sq_rm1[:, c],
                op0=ALU.mult, op1=ALU.mult,
            )

        def moebius_6(rows):
            c = cols(rows)
            nc.vector.scalar_tensor_tensor(
                out=sum_den[:, c], in0=sum_sq[:, c], scalar=SUM_SQ_MIN, in1=den[:, c],
                op0=ALU.max, op1=ALU.mult,
            )

        def root_of_r2(rows):
            power(sum_den_rsqrt, sum_den, neg_half, rows)

        def norm_and_unit_of_r2(rows):
            for i in rows:
                nc.vector.tensor_scalar(
                    out=col(r2_clip, i), in0=col(sum_sq, i), scalar1=col(sum_den_rsqrt, i),
                    scalar2=BOUND, op0=ALU.mult, op1=ALU.min,
                )
                nc.vector.tensor_scalar(
                    out=col(half_unit, i), in0=col(r_sq_m1, i), scalar1=-0.5,
                    scalar2=col(sum_den_rsqrt, i), op0=ALU.mult, op1=ALU.mult,
                )

        def log_of_r2(rows):
            c = cols(rows)
            nc.scalar.activation(out=ln_up2[:, c], in_=r2_clip[:, c], func=ACT.Ln, bias=1.0, scale=1.0)
            nc.scalar.activation(out=ln_dn2[:, c], in_=r2_clip[:, c], func=ACT.Ln, bias=1.0, scale=-1.0)

        def log_map_coefficient(rows):
            for i in rows:
                nc.vector.tensor_scalar(
                    out=col(log_coef, i), in0=col(ln_up2, i), scalar1=col(ln_dn2, i),
                    scalar2=col(half_unit, i), op0=ALU.subtract, op1=ALU.mult,
                )

        z = per_tile([P, D], F32, "z")
        relu_sq = row_numbers("relu_sq")
        relu_norm = row_numbers("relu_norm")

        def direction(i):
            nc.vector.scalar_tensor_tensor(
                out=z[i][:], in0=xt[i][:], scalar=col(xt_share, i), in1=y_bc[:],
                op0=ALU.mult, op1=ALU.add,
            )

        def relu_square_sum(i):
            products = scrap.tile([P, D], F32, name="products")
            nc.vector.scalar_tensor_tensor(
                out=products[:], in0=z[i][:], scalar=0.0, in1=z[i][:],
                op0=ALU.max, op1=ALU.mult, accum_out=col(relu_sq, i),
            )

        relu_z = {}

        def relu_on_scalar(i):
            relu_z[i] = scrap.tile([P, D], F32, name="relu_z")
            nc.scalar.activation(out=relu_z[i][:], in_=z[i][:], func=ACT.Relu)

        def relu_square_sum_on_scalar(i):
            square_sum(relu_z[i][:], col(relu_sq, i))

        v_tanh = row_numbers("v_tanh")
        relu_rnorm = row_numbers("relu_rnorm")
        out_coef = row_numbers("out_coef")
        result = per_tile([P, D], F32, "result")

        def norm_of_relu(rows):
            power(relu_norm, relu_sq, half, rows)

        def tanh_of_v(rows):
            for i in rows:
                nc.scalar.activation(
                    out=col(v_tanh, i), in_=col(relu_norm, i), func=ACT.Tanh,
                    scale=col(log_coef, i),
                )

        def reciprocal_of_relu(rows):
            c = cols(rows)
            nc.vector.reciprocal(out=relu_rnorm[:, c], in_=relu_norm[:, c])

        def out_coefficient(rows):
            for i in rows:
                nc.vector.tensor_scalar(
                    out=col(out_coef, i), in0=col(relu_rnorm, i), scalar1=1.0 / NORM_MIN,
                    scalar2=col(v_tanh, i), op0=ALU.min, op1=ALU.mult,
                )

        def store(i):
            nc.sync.dma_start(out=out[i * P : (i + 1) * P, :], in_=result[i][:])

        def finish_on_scalar(i):
            nc.scalar.activation(out=result[i][:], in_=z[i][:], func=ACT.Relu, scale=col(out_coef, i))
            store(i)

        def finish(i):
            nc.vector.tensor_scalar(
                out=result[i][:], in0=z[i][:], scalar1=0.0, scalar2=col(out_coef, i),
                op0=ALU.max, op1=ALU.mult,
            )
            store(i)

        ALL = range(TILES)
        A = range(0, 2)
        B = range(2, 4)

        spread(gamma_col, affine_ps[:, 0])
        shifted_square_sum(0)
        shifted_sum(0)
        first_terms(A)
        first_terms(B)
        shifted_square_sum(1)
        shifted_sum(1)
        terms_of_h(0, nc.vector)
        mean_of_h(0)
        terms_of_h(1, nc.vector)
        clip_of_h(0, nc.vector)
        mean_of_h(1)
        clip_of_h(1, nc.vector)
        root_of_h(A)
        shifted_square_sum(2)
        shifted_sum(2)
        deviation_of_h(0)
        deviation_of_h(1)
        shifted_square_sum(3)
        shifted_sum(3)
        spread(beta_col, affine_ps[:, 1])
        transpose_weight(0)
        transpose_weight(1)
        bias_square_sum()
        spread_bias()
        log_of_h(A)
        terms_of_h(2, nc.vector)
        terms_of_h(3, nc.vector)
        mean_of_h(2)
        clip_of_h(2, nc.vector)
        clip_of_h(3, nc.vector)
        mean_of_h(3)
        root_of_h(B)
        root_of_k(A)
        deviation_of_h(2)
        deviation_of_h(3)
        regroup_weight(0)
        centre(0)
        centre(1)
        bias_clip()
        log_of_h(B)
        layer_norm_factor(A)
        root_of_k(B)
        bias_root()
        bias_exponential()
        centre(2)
        centre(3)
        regroup_weight(1)
        layer_norm(0)
        layer_norm(1)
        layer_norm_factor(B)
        square_sum_of_x(0)
        layer_norm(2)
        square_sum_of_x(1)
        norm_of_x(A)
        layer_norm(3)
        bias_tanh_1()
        square_sum_of_x(2)
        square_sum_of_x(3)
        norm_of_x(B)
        load_table(ACT.Tanh, "warm_tanh_a", col(x_sq, 3))
        quantise_weight()
        bias_tanh_2()
        shrink_factor(A)
        bias_tanh_3()
        make_u(0)
        transpose_u(0)
        make_u(1)
        scale_of_y()
        transpose_u(1)
        shrink_factor(B)
        make_u(2)
        transpose_u(2)
        make_u(3)
        transpose_u(3)
        regroup_u(0)
        quantise_u(0)
        multiply(0)
        regroup_u(1)
        collect_y()
        quantise_u(1)
        multiply(1)
        regroup_u_on_vector(2)
        regroup_u_on_vector(3)
        quantise_u(2)
        multiply(2)
        quantise_u(3)
        multiply(3)
        bias_squares()
        square_sum_of_xt(0)
        square_sum_of_xt(1)
        norm_of_xt(A)
        dot_with_y(0)
        square_sum_of_xt(2)
        dot_with_y(1)
        square_sum_of_xt(3)
        norm_of_xt(B)
        dot_with_y(2)
        tanh_of_norm(ALL)
        load_table(ACT.Ln, "warm_ln_b", col(r_norm, 3))
        dot_with_y(3)
        moebius_1(ALL)
        moebius_2(ALL)
        moebius_3(ALL)
        moebius_4(ALL)
        moebius_5(ALL)
        moebius_6(ALL)
        root_of_r2(A)
        root_of_r2(B)
        direction(0)
        relu_on_scalar(0)
        direction(1)
        relu_square_sum_on_scalar(0)
        norm_and_unit_of_r2(A)
        direction(2)
        norm_and_unit_of_r2(B)
        log_of_r2(ALL)
        load_table(ACT.Tanh, "warm_tanh_b", col(ln_dn2, 3))
        relu_square_sum(1)
        norm_of_relu(A)
        direction(3)
        log_map_coefficient(A)
        tanh_of_v(A)
        relu_square_sum(2)
        reciprocal_of_relu(A)
        relu_square_sum(3)
        norm_of_relu(B)
        out_coefficient(A)
        log_map_coefficient(B)
        finish(0)
        finish_on_scalar(1)
        tanh_of_v(B)
        reciprocal_of_relu(B)
        out_coefficient(B)
        finish(2)
        finish_on_scalar(3)
